import numpy as np
import ml_dtypes


def mxq(x, axis, fmt="e4m3"):
    dtype, down = {"e4m3": (ml_dtypes.float8_e4m3fn, 7), "e5m2": (ml_dtypes.float8_e5m2, 14)}[fmt]
    v = np.moveaxis(np.asarray(x, np.float32).astype(ml_dtypes.bfloat16).astype(np.float64), axis, -1)
    blocks = v.reshape(v.shape[:-1] + (-1, 32))
    amax = np.abs(blocks).max(-1, keepdims=True)
    byte = np.maximum(np.where(amax > 0, np.frexp(amax)[1] - 1 + 127, 0) - down, 1)
    scale = np.exp2(byte - 127.0)
    codes = (blocks / scale).astype(np.float32).astype(dtype).astype(np.float64)
    return np.moveaxis((codes * scale).reshape(v.shape), -1, axis)


WIDE = False


def mx_kscale(k):
    if not WIDE:
        return np.ones(k)
    levels = np.array([10, -10, 5, -5, 0])
    a = np.random.permutation(np.resize(levels, k // 512 * 4)).reshape(k // 512, 4)
    idx = np.arange(k)
    return np.exp2(a[idx // 512, idx % 128 // 32])


BF16 = ml_dtypes.bfloat16


def bf(x):
    return np.asarray(x, np.float32).astype(BF16)


def f64(x):
    return np.asarray(x).astype(np.float64)


N, C, O, TH, TW = 2, 16384, 256, 8, 16
BN_EPS = 1e-5
IMG_SIZES = [(max(TH >> (l + 1), 1), max(TW >> (l + 1), 1)) for l in range(5)]


def setup_inputs():
    s = mx_kscale(C)
    sc = s[None, :, None, None]
    inp = {}
    for l, (h, w) in enumerate(IMG_SIZES):
        inp[f'img_feat{l}'] = bf(np.random.standard_normal((N, C, h, w)) * 0.5 * sc)
    inp['pts_feat0'] = bf(np.random.standard_normal((N, C, TH, TW)) * sc)
    inp['img_w'] = bf(np.random.standard_normal((O, C)) / np.sqrt(C) / s[None, :])
    inp['img_b'] = bf(np.random.standard_normal(O) * 0.1)
    inp['img_gamma'] = bf(1.0 + 0.1 * np.random.standard_normal(O))
    inp['img_beta'] = bf(np.random.standard_normal(O) * 0.1)
    inp['img_mean'] = bf(np.random.standard_normal(O) * 0.1)
    inp['img_var'] = bf(np.random.uniform(0.5, 1.5, O))
    inp['pts_w'] = bf(np.random.standard_normal((O, C)) / np.sqrt(C) / s[None, :])
    inp['pts_b'] = bf(np.random.standard_normal(O) * 0.1)
    inp['pts_gamma'] = bf(1.0 + 0.1 * np.random.standard_normal(O))
    inp['pts_beta'] = bf(np.random.standard_normal(O) * 0.1)
    inp['pts_mean'] = bf(np.random.standard_normal(O) * 0.1)
    inp['pts_var'] = bf(np.random.uniform(0.5, 1.5, O))
    return inp


def _obtain_mlvl(feats, th, tw):
    n = feats[0].shape[0]
    outs = []
    for i in range(n):
        acc = None
        for lvl, f in enumerate(feats):
            x = f[i]
            if lvl > 0:
                s = i + 1
                x = np.repeat(np.repeat(x, s, axis=1), s, axis=2)
            dh = th - x.shape[1]
            dw = tw - x.shape[2]
            x = np.pad(x, ((0, 0), (dh // 2, dh - dh // 2), (dw // 2, dw - dw // 2)), mode='edge')
            acc = x if acc is None else acc + x
        outs.append(acc)
    return np.stack(outs, 0)


def _conv_bn_relu(x, w, b, gamma, beta, mean, var):
    n, c, h, wd = x.shape
    y = (mxq(w, 1, 'e4m3') @ mxq(x, 1, 'e4m3').reshape(n, c, h * wd)).reshape(n, -1, h, wd) + b[None, :, None, None]
    scale = gamma / np.sqrt(var + BN_EPS)
    y = (y - mean[None, :, None, None]) * scale[None, :, None, None] + beta[None, :, None, None]
    return np.maximum(y, 0.0)


def reference(img_feat0, img_feat1, img_feat2, img_feat3, img_feat4, pts_feat0,
              img_w, img_b, img_gamma, img_beta, img_mean, img_var,
              pts_w, pts_b, pts_gamma, pts_beta, pts_mean, pts_var):
    th, tw = pts_feat0.shape[2], pts_feat0.shape[3]
    pts_m = _obtain_mlvl([f64(pts_feat0)], th, tw)
    pts_pre = _conv_bn_relu(pts_m, f64(pts_w), f64(pts_b), f64(pts_gamma), f64(pts_beta), f64(pts_mean), f64(pts_var))
    img_m = _obtain_mlvl([f64(img_feat0), f64(img_feat1), f64(img_feat2), f64(img_feat3), f64(img_feat4)], th, tw)
    img_pre = _conv_bn_relu(img_m, f64(img_w), f64(img_b), f64(img_gamma), f64(img_beta), f64(img_mean), f64(img_var))
    return np.concatenate((img_pre, pts_pre), axis=1)

@@ -1,0 +1,404 @@
+from contextlib import ExitStack
+
+import concourse.mybir as mybir
+from concourse.masks import make_identity
+
+BF16 = mybir.dt.bfloat16
+F32 = mybir.dt.float32
+I32 = mybir.dt.int32
+U32 = mybir.dt.uint32
+U8 = mybir.dt.uint8
+FP8X4 = mybir.dt.float8_e4m3fn_x4
+ADD = mybir.AluOpType.add
+RELU = mybir.ActivationFunctionType.Relu
+
+P = 128
+PACK = 4
+K_PASS = P * PACK
+
+SAMPLES = 2
+CHANNELS = 16384
+OUT_CH = 256
+O_HALVES = OUT_CH // P
+TH, TW = 8, 16
+POSITIONS = TH * TW
+GRID_H, GRID_W = 4, 8
+GRID_TOP, GRID_LEFT = (TH - GRID_H) // 2, (TW - GRID_W) // 2
+GRID = GRID_H * GRID_W
+L1_H, L1_W = 2, 4
+L2_W = 2
+BN_EPS = 1e-5
+
+PASSES = CHANNELS // K_PASS
+CHUNK_PASSES = 4
+CHUNK_CH = CHUNK_PASSES * K_PASS
+CHUNKS = PASSES // CHUNK_PASSES
+RUN = 2 * P
+RUNS = CHANNELS // RUN
+
+MIN_MOVING = 128
+
+FLOPS = 2 * 2 * OUT_CH * CHANNELS * SAMPLES * POSITIONS
+
+
+def padded_source(index, size, level_size, repeat):
+    length = level_size * repeat
+    before = (size - length) // 2
+    return min(max(index - before, 0), length - 1) // repeat
+
+
+def grid_row(h):
+    return min(max(h, GRID_TOP), GRID_TOP + GRID_H - 1)
+
+
+def grid_col(w):
+    return min(max(w, GRID_LEFT), GRID_LEFT + GRID_W - 1)
+
+
+assert all(
+    padded_source(h, TH, L1_H, rep) == padded_source(grid_row(h), TH, L1_H, rep)
+    for rep in (1, 2)
+    for h in range(TH)
+)
+assert all(
+    padded_source(w, TW, size, rep) == padded_source(grid_col(w), TW, size, rep)
+    for rep in (1, 2)
+    for size in (L1_W, L2_W)
+    for w in range(TW)
+)
+assert all(
+    padded_source(w, TW, L2_W, rep) == padded_source(w, TW, L1_W, rep) // 2
+    for rep in (1, 2)
+    for w in range(TW)
+)
+
+
+def load_weight_chunk(nc, raw, w, chunk):
+    w_raw = raw.tile([P, O_HALVES, CHUNK_CH], BF16)
+    channels = slice(chunk * CHUNK_CH, (chunk + 1) * CHUNK_CH)
+    nc.sync.dma_start(
+        out=w_raw[:], in_=w[:, channels].rearrange("(h o) c -> o h c", h=O_HALVES)
+    )
+    return w_raw
+
+
+def transpose_weight_chunk(nc, banks, work, ident, w_raw):
+    w_words = w_raw[:].bitcast(F32)
+    w_grouped = work.tile([P, CHUNK_PASSES, OUT_CH, PACK], BF16, align_bytes=64)
+    grouped_words = w_grouped[:].bitcast(F32)
+    for g in range(CHUNK_PASSES):
+        bank = banks.tile([P, O_HALVES, 2, P], F32)
+        for h in range(O_HALVES):
+            for u in range(2):
+                first = (2 * g + u) * P
+                nc.tensor.transpose(bank[:, h, u, :], w_words[:, h, first : first + P], ident[:])
+        nc.scalar.copy(
+            out=grouped_words[:, g].rearrange("p (h o) u -> p h o u", h=O_HALVES),
+            in_=bank[:].rearrange("p h u o -> p h o u"),
+        )
+    return w_grouped
+
+
+def load_pts_chunk(nc, raw, pts_feat0, chunk):
+    pts_raw = raw.tile([P, SAMPLES, CHUNK_PASSES * PACK, POSITIONS], BF16)
+    channels = slice(chunk * CHUNK_CH, (chunk + 1) * CHUNK_CH)
+    for n in range(SAMPLES):
+        nc.sync.dma_start(
+            out=pts_raw[:, n].rearrange("p (m e) s -> p m (e s)", e=2),
+            in_=pts_feat0[n, channels].rearrange("(m p e) h w -> p m (e h w)", p=P, e=2),
+        )
+    return pts_raw
+
+
+def regroup_pts_chunk(nc, work, pts_raw):
+    pts_grouped = work.tile([P, CHUNK_PASSES, SAMPLES * POSITIONS, PACK], BF16, align_bytes=64)
+    for n in range(SAMPLES):
+        nc.vector.tensor_copy(
+            out=pts_grouped[:, :, n * POSITIONS : (n + 1) * POSITIONS, :].rearrange(
+                "p g (c i) t -> p g c t i", i=4
+            ),
+            in_=pts_raw[:, n].rearrange("p (g t) (c i) -> p g c t i", t=PACK, i=4),
+        )
+    return pts_grouped
+
+
+def quantise_chunk(nc, grouped, codes, scales):
+    nc.vector.quantize_mx(
+        out=codes.rearrange("p g c -> p (g c)").bitcast(FP8X4),
+        scales=scales.rearrange("p g c -> p (g c)"),
+        in_=grouped[:].rearrange("p g c t -> p (g c t)"),
+    )
+
+
+def tile_prefusioncat_k_kernel(
+    tc,
+    img_feat0,
+    img_feat1,
+    img_feat2,
+    img_feat3,
+    img_feat4,
+    pts_feat0,
+    img_w,
+    img_b,
+    img_gamma,
+    img_beta,
+    img_mean,
+    img_var,
+    pts_w,
+    pts_b,
+    pts_gamma,
+    pts_beta,
+    pts_mean,
+    pts_var,
+    out,
+):
+    nc = tc.nc
+    with ExitStack() as pools:
+        const = pools.enter_context(tc.tile_pool(name="const", bufs=1))
+        img = pools.enter_context(tc.tile_pool(name="img", bufs=1))
+        w_in = pools.enter_context(tc.tile_pool(name="w_in", bufs=4))
+        pts_in = pools.enter_context(tc.tile_pool(name="pts_in", bufs=3))
+        work = pools.enter_context(tc.tile_pool(name="work", bufs=2))
+        results = pools.enter_context(tc.tile_pool(name="results", bufs=2))
+        banks = pools.enter_context(tc.psum_pool(name="banks", bufs=5))
+        sums = pools.enter_context(tc.psum_pool(name="sums", bufs=1))
+
+        ident = const.tile([P, P], F32)
+        make_identity(nc, ident[:])
+
+        vectors = (
+            (img_b, img_gamma, img_beta, img_mean, img_var),
+            (pts_b, pts_gamma, pts_beta, pts_mean, pts_var),
+        )
+        vec_rows = const.tile([P, P], BF16)
+        nc.vector.memset(vec_rows[:], 0.0)
+        for b in range(2):
+            for v in range(5):
+                row = (b * 5 + v) * O_HALVES
+                nc.gpsimd.dma_start(
+                    out=vec_rows[row : row + O_HALVES, :],
+                    in_=vectors[b][v].rearrange("(h o) -> h o", h=O_HALVES),
+                )
+        vec_rows_f32 = const.tile([P, P], F32)
+        nc.vector.tensor_copy(out=vec_rows_f32[:], in_=vec_rows[:])
+        vec_bank = banks.tile([P, O_HALVES, 2, P], F32, tag="bank")
+        nc.tensor.transpose(vec_bank[:, 0, 0, :], vec_rows_f32[:], ident[:])
+        vec = const.tile([P, 2, 5, O_HALVES], F32)
+        nc.vector.tensor_copy(
+            out=vec[:].rearrange("p b v h -> p (b v h)"), in_=vec_bank[:, 0, 0, 0 : 2 * 5 * O_HALVES]
+        )
+        bias, gamma, beta, mean, var = (vec[:, :, v, :] for v in range(5))
+        var_eps = const.tile([P, 2, O_HALVES], F32)
+        nc.vector.tensor_scalar_add(out=var_eps[:], in0=var, scalar1=BN_EPS)
+        std = const.tile([P, 2, O_HALVES], F32)
+        nc.scalar.sqrt(out=std[:], in_=var_eps[:])
+        inv_std = const.tile([P, 2, O_HALVES], F32)
+        nc.vector.reciprocal(out=inv_std[:], in_=std[:])
+        bn_scale = const.tile([P, 2, O_HALVES], F32)
+        nc.vector.tensor_mul(out=bn_scale[:], in0=gamma, in1=inv_std[:])
+        centred = const.tile([P, 2, O_HALVES], F32)
+        nc.vector.tensor_sub(out=centred[:], in0=bias, in1=mean)
+        scaled = const.tile([P, 2, O_HALVES], F32)
+        nc.vector.tensor_mul(out=scaled[:], in0=centred[:], in1=bn_scale[:])
+        bn_shift = const.tile([P, 2, O_HALVES], F32)
+        nc.vector.tensor_add(out=bn_shift[:], in0=scaled[:], in1=beta)
+
+        l1_raw = img.tile([P, RUN, L1_H * L1_W], BF16)
+        nc.sync.dma_start(
+            out=l1_raw[:], in_=img_feat1.rearrange("n (m q) h w -> (n m) q (h w)", q=RUN)
+        )
+        l2_raw = img.tile([P, RUN, L2_W], BF16)
+        nc.sync.dma_start(
+            out=l2_raw[:], in_=img_feat2.rearrange("n (m q) h w -> (n m) q (h w)", q=RUN)
+        )
+        l3_raw = img.tile([P, RUN], BF16)
+        nc.sync.dma_start(
+            out=l3_raw[:], in_=img_feat3.rearrange("n (m q) h w -> (n m) (q h w)", q=RUN)
+        )
+        l4_raw = img.tile([P, RUN], BF16)
+        nc.sync.dma_start(
+            out=l4_raw[:], in_=img_feat4.rearrange("n (m q) h w -> (n m) (q h w)", q=RUN)
+        )
+        l0_raw = img.tile([P, SAMPLES, PASSES * PACK, GRID], BF16)
+        for n in range(SAMPLES):
+            nc.sync.dma_start(
+                out=l0_raw[:, n].rearrange("p (m e) s -> p m (e s)", e=2),
+                in_=img_feat0[n].rearrange("(m p e) h w -> p m (e h w)", p=P, e=2),
+            )
+
+        sum34 = img.tile([P, RUN], F32)
+        nc.vector.tensor_tensor(out=sum34[:], in0=l3_raw[:], in1=l4_raw[:], op=ADD)
+        sum234 = img.tile([P, RUN, L2_W], F32)
+        nc.vector.tensor_tensor(
+            out=sum234[:],
+            in0=l2_raw[:],
+            in1=sum34[:].unsqueeze(2).to_broadcast([P, RUN, L2_W]),
+            op=ADD,
+        )
+        lower = img.tile([P, L1_H, L1_W, 2, P], F32)
+        l1_view = l1_raw[:].rearrange("p (x e) (r d k) -> p r e d k x", e=2, r=L1_H, d=L2_W)
+        sum234_view = sum234[:].rearrange("p (x e) d -> p e d x", e=2)
+        for r in range(L1_H):
+            for e in range(2):
+                nc.vector.tensor_tensor(
+                    out=lower[:, r, :, e, :].rearrange("p (d k) x -> p d k x", d=L2_W),
+                    in0=l1_view[:, r, e],
+                    in1=sum234_view[:, e].unsqueeze(2).to_broadcast([P, L2_W, L1_W // L2_W, P]),
+                    op=ADD,
+                )
+        lower_t = img.tile([P, L1_H, L1_W, SAMPLES, PASSES, PACK], F32)
+        for r in range(L1_H):
+            for d in range(L2_W):
+                pair = slice(2 * d, 2 * d + 2)
+                lower_bank = banks.tile([P, 2, 2, P], F32, tag="bank")
+                for k in range(2):
+                    for e in range(2):
+                        nc.tensor.transpose(
+                            lower_bank[:, k, e, :], lower[:, r, 2 * d + k, e, :], ident[:]
+                        )
+                nc.scalar.copy(
+                    out=lower_t[:, r, pair].rearrange("p k n g (u e) -> p k (n g u) e", e=2),
+                    in_=lower_bank[:].rearrange("p k e q -> p k q e"),
+                )
+        img_grouped = img.tile([P, PASSES, SAMPLES * GRID, PACK], BF16, align_bytes=64)
+        l0_view = l0_raw[:].rearrange("p n (g t) s -> p n g s t", t=PACK)
+        for n in range(SAMPLES):
+            for i in range(GRID_H):
+                r = padded_source(GRID_TOP + i, TH, L1_H, n + 1)
+                for c in range(L1_W):
+                    cols = [
+                        j
+                        for j in range(GRID_W)
+                        if padded_source(GRID_LEFT + j, TW, L1_W, n + 1) == c
+                    ]
+                    first = i * GRID_W + cols[0]
+                    nc.vector.tensor_tensor(
+                        out=img_grouped[:, :, n * GRID + first : n * GRID + first + len(cols), :],
+                        in0=l0_view[:, n, :, first : first + len(cols), :],
+                        in1=lower_t[:, r, c, n]
+                        .unsqueeze(2)
+                        .to_broadcast([P, PASSES, len(cols), PACK]),
+                        op=ADD,
+                    )
+        img_cols = SAMPLES * GRID
+        img_codes = img.tile([P, PASSES * img_cols + MIN_MOVING - img_cols], U32, align_bytes=64)
+        img_scales = img.tile([P, PASSES * img_cols + MIN_MOVING - img_cols], U8, align_bytes=64)
+        nc.vector.memset(img_codes[:, PASSES * img_cols :].bitcast(I32), 0)
+        nc.vector.memset(img_scales[:, PASSES * img_cols :].bitcast(I32), 0)
+        half = PASSES // 2
+        for part in range(2):
+            nc.vector.quantize_mx(
+                out=img_codes[:, part * half * img_cols : (part + 1) * half * img_cols].bitcast(
+                    FP8X4
+                ),
+                scales=img_scales[:, part * half * img_cols : (part + 1) * half * img_cols],
+                in_=img_grouped[:, part * half : (part + 1) * half].rearrange(
+                    "p g c t -> p (g c t)"
+                ),
+            )
+
+        img_w_codes = img.tile([P, PASSES, OUT_CH], U32, align_bytes=64)
+        img_w_scales = img.tile([P, PASSES, OUT_CH], U8, align_bytes=64)
+        for chunk in range(CHUNKS):
+            w_raw = load_weight_chunk(nc, w_in, img_w, chunk)
+            w_grouped = transpose_weight_chunk(nc, banks, work, ident, w_raw)
+            passes = slice(chunk * CHUNK_PASSES, (chunk + 1) * CHUNK_PASSES)
+            quantise_chunk(nc, w_grouped, img_w_codes[:, passes], img_w_scales[:, passes])
+
+        img_sum = sums.tile([P, O_HALVES, MIN_MOVING], F32)
+        for h in range(O_HALVES):
+            o_cols = slice(h * P, (h + 1) * P)
+            for g in range(PASSES):
+                moving = slice(g * img_cols, g * img_cols + MIN_MOVING)
+                nc.tensor.matmul_mx(
+                    out=img_sum[:, h, :],
+                    lhsT=img_w_codes[:, g, o_cols].bitcast(FP8X4),
+                    lhsT_scale=img_w_scales[:, g, o_cols],
+                    rhs=img_codes[:, moving].bitcast(FP8X4),
+                    rhs_scale=img_scales[:, moving],
+                    start=(g == 0),
+                    stop=(g == PASSES - 1),
+                )
+        for h in range(O_HALVES):
+            grid = img_sum[:, h, 0:img_cols].rearrange(
+                "p (n i j) -> p n i j", n=SAMPLES, i=GRID_H
+            )
+            img_res = results.tile([P, SAMPLES, TH, TW], F32)
+            rows = slice(GRID_TOP, GRID_TOP + GRID_H)
+            right = GRID_LEFT + GRID_W
+            for dst_cols, src in (
+                (slice(GRID_LEFT, right), grid),
+                (slice(0, GRID_LEFT), grid[:, :, :, 0:1]),
+                (slice(right, TW), grid[:, :, :, GRID_W - 1 : GRID_W]),
+            ):
+                dst = img_res[:, :, rows, dst_cols]
+                nc.scalar.activation(
+                    out=dst,
+                    in_=src.to_broadcast(dst.shape),
+                    func=RELU,
+                    bias=bn_shift[:, 0, h : h + 1],
+                    scale=bn_scale[:, 0, h : h + 1],
+                )
+            nc.scalar.copy(
+                out=img_res[:, :, 0:GRID_TOP, :],
+                in_=img_res[:, :, GRID_TOP : GRID_TOP + 1, :].to_broadcast(
+                    [P, SAMPLES, GRID_TOP, TW]
+                ),
+            )
+            bottom = GRID_TOP + GRID_H
+            nc.scalar.copy(
+                out=img_res[:, :, bottom:TH, :],
+                in_=img_res[:, :, bottom - 1 : bottom, :].to_broadcast(
+                    [P, SAMPLES, TH - bottom, TW]
+                ),
+            )
+            nc.sync.dma_start(
+                out=out[:, h * P : (h + 1) * P].rearrange("n o h w -> o n (h w)"),
+                in_=img_res[:].rearrange("p n h w -> p n (h w)"),
+            )
+
+        pts_sums = [
+            sums.tile([P, SAMPLES * POSITIONS], F32, name="pts_sum%d" % h) for h in range(O_HALVES)
+        ]
+        operands = {}
+        for chunk in range(CHUNKS + 1):
+            if chunk < CHUNKS:
+                w_raw = load_weight_chunk(nc, w_in, pts_w, chunk)
+                pts_raw = load_pts_chunk(nc, pts_in, pts_feat0, chunk)
+                w_grouped = transpose_weight_chunk(nc, banks, work, ident, w_raw)
+                pts_grouped = regroup_pts_chunk(nc, work, pts_raw)
+                w_codes = work.tile([P, CHUNK_PASSES, OUT_CH], U32, align_bytes=64)
+                w_scales = work.tile([P, CHUNK_PASSES, OUT_CH], U8, align_bytes=64)
+                quantise_chunk(nc, w_grouped, w_codes[:], w_scales[:])
+                pts_codes = work.tile([P, CHUNK_PASSES, SAMPLES * POSITIONS], U32, align_bytes=64)
+                pts_scales = work.tile([P, CHUNK_PASSES, SAMPLES * POSITIONS], U8, align_bytes=64)
+                quantise_chunk(nc, pts_grouped, pts_codes[:], pts_scales[:])
+                operands[chunk] = (w_codes, w_scales, pts_codes, pts_scales)
+            if chunk > 0:
+                w_codes, w_scales, pts_codes, pts_scales = operands[chunk - 1]
+                for g in range(CHUNK_PASSES):
+                    done = (chunk - 1) * CHUNK_PASSES + g
+                    for h in range(O_HALVES):
+                        o_cols = slice(h * P, (h + 1) * P)
+                        nc.tensor.matmul_mx(
+                            out=pts_sums[h][:],
+                            lhsT=w_codes[:, g, o_cols].bitcast(FP8X4),
+                            lhsT_scale=w_scales[:, g, o_cols],
+                            rhs=pts_codes[:, g, :].bitcast(FP8X4),
+                            rhs_scale=pts_scales[:, g, :],
+                            start=(done == 0),
+                            stop=(done == PASSES - 1),
+                        )
+        for h in range(O_HALVES):
+            pts_res = results.tile([P, SAMPLES, POSITIONS], F32)
+            nc.scalar.activation(
+                out=pts_res[:].rearrange("p n s -> p (n s)"),
+                in_=pts_sums[h][:],
+                func=RELU,
+                bias=bn_shift[:, 1, h : h + 1],
+                scale=bn_scale[:, 1, h : h + 1],
+            )
+            nc.sync.dma_start(
+                out=out[:, OUT_CH + h * P : OUT_CH + (h + 1) * P].rearrange("n o h w -> o n (h w)"),
+                in_=pts_res[:],
+            )

@@ -179,29 +179,6 @@ def tile_prefusioncat_k_kernel(
                     out=vec_rows[row : row + O_HALVES, :],
                     in_=vectors[b][v].rearrange("(h o) -> h o", h=O_HALVES),
                 )
-        vec_rows_f32 = const.tile([P, P], F32)
-        nc.vector.tensor_copy(out=vec_rows_f32[:], in_=vec_rows[:])
-        vec_bank = banks.tile([P, O_HALVES, 2, P], F32, tag="bank")
-        nc.tensor.transpose(vec_bank[:, 0, 0, :], vec_rows_f32[:], ident[:])
-        vec = const.tile([P, 2, 5, O_HALVES], F32)
-        nc.vector.tensor_copy(
-            out=vec[:].rearrange("p b v h -> p (b v h)"), in_=vec_bank[:, 0, 0, 0 : 2 * 5 * O_HALVES]
-        )
-        bias, gamma, beta, mean, var = (vec[:, :, v, :] for v in range(5))
-        var_eps = const.tile([P, 2, O_HALVES], F32)
-        nc.vector.tensor_scalar_add(out=var_eps[:], in0=var, scalar1=BN_EPS)
-        std = const.tile([P, 2, O_HALVES], F32)
-        nc.scalar.sqrt(out=std[:], in_=var_eps[:])
-        inv_std = const.tile([P, 2, O_HALVES], F32)
-        nc.vector.reciprocal(out=inv_std[:], in_=std[:])
-        bn_scale = const.tile([P, 2, O_HALVES], F32)
-        nc.vector.tensor_mul(out=bn_scale[:], in0=gamma, in1=inv_std[:])
-        centred = const.tile([P, 2, O_HALVES], F32)
-        nc.vector.tensor_sub(out=centred[:], in0=bias, in1=mean)
-        scaled = const.tile([P, 2, O_HALVES], F32)
-        nc.vector.tensor_mul(out=scaled[:], in0=centred[:], in1=bn_scale[:])
-        bn_shift = const.tile([P, 2, O_HALVES], F32)
-        nc.vector.tensor_add(out=bn_shift[:], in0=scaled[:], in1=beta)
 
         l1_raw = img.tile([P, RUN, L1_H * L1_W], BF16)
         nc.sync.dma_start(
@@ -304,6 +281,30 @@ def tile_prefusioncat_k_kernel(
             w_grouped = transpose_weight_chunk(nc, banks, work, ident, w_raw)
             passes = slice(chunk * CHUNK_PASSES, (chunk + 1) * CHUNK_PASSES)
             quantise_chunk(nc, w_grouped, img_w_codes[:, passes], img_w_scales[:, passes])
+
+        vec_rows_f32 = const.tile([P, P], F32)
+        nc.vector.tensor_copy(out=vec_rows_f32[:], in_=vec_rows[:])
+        vec_bank = banks.tile([P, O_HALVES, 2, P], F32, tag="bank")
+        nc.tensor.transpose(vec_bank[:, 0, 0, :], vec_rows_f32[:], ident[:])
+        vec = const.tile([P, 2, 5, O_HALVES], F32)
+        nc.vector.tensor_copy(
+            out=vec[:].rearrange("p b v h -> p (b v h)"), in_=vec_bank[:, 0, 0, 0 : 2 * 5 * O_HALVES]
+        )
+        bias, gamma, beta, mean, var = (vec[:, :, v, :] for v in range(5))
+        var_eps = const.tile([P, 2, O_HALVES], F32)
+        nc.vector.tensor_scalar_add(out=var_eps[:], in0=var, scalar1=BN_EPS)
+        std = const.tile([P, 2, O_HALVES], F32)
+        nc.scalar.sqrt(out=std[:], in_=var_eps[:])
+        inv_std = const.tile([P, 2, O_HALVES], F32)
+        nc.vector.reciprocal(out=inv_std[:], in_=std[:])
+        bn_scale = const.tile([P, 2, O_HALVES], F32)
+        nc.vector.tensor_mul(out=bn_scale[:], in0=gamma, in1=inv_std[:])
+        centred = const.tile([P, 2, O_HALVES], F32)
+        nc.vector.tensor_sub(out=centred[:], in0=bias, in1=mean)
+        scaled = const.tile([P, 2, O_HALVES], F32)
+        nc.vector.tensor_mul(out=scaled[:], in0=centred[:], in1=bn_scale[:])
+        bn_shift = const.tile([P, 2, O_HALVES], F32)
+        nc.vector.tensor_add(out=bn_shift[:], in0=scaled[:], in1=beta)
 
         img_sum = sums.tile([P, O_HALVES, MIN_MOVING], F32)
         for h in range(O_HALVES):

@@ -353,7 +353,7 @@ def tile_prefusioncat_k_kernel(
                     [P, SAMPLES, TH - bottom, TW]
                 ),
             )
-            nc.sync.dma_start(
+            nc.scalar.dma_start(
                 out=out[:, h * P : (h + 1) * P].rearrange("n o h w -> o n (h w)"),
                 in_=img_res[:].rearrange("p n h w -> p n (h w)"),
             )

@@ -33,10 +33,13 @@ PASSES = CHANNELS // K_PASS
 CHUNK_PASSES = 4
 CHUNK_CH = CHUNK_PASSES * K_PASS
 CHUNKS = PASSES // CHUNK_PASSES
+PASS_WORDS = K_PASS // 2
 RUN = 2 * P
-RUNS = CHANNELS // RUN
 
 MIN_MOVING = 128
+
+WORDS_IN_HALVES = "o (u p) -> o u p"
+WORDS_ALTERNATING = "o (p u) -> o u p"
 
 FLOPS = 2 * 2 * OUT_CH * CHANNELS * SAMPLES * POSITIONS
 
@@ -82,16 +85,18 @@ def load_weight_chunk(nc, raw, w, chunk):
     return w_raw
 
 
-def transpose_weight_chunk(nc, banks, work, ident, w_raw):
+def transpose_weight_chunk(nc, banks, work, ident, w_raw, word_order):
     w_words = w_raw[:].bitcast(F32)
     w_grouped = work.tile([P, CHUNK_PASSES, OUT_CH, PACK], BF16, align_bytes=64)
     grouped_words = w_grouped[:].bitcast(F32)
     for g in range(CHUNK_PASSES):
         bank = banks.tile([P, O_HALVES, 2, P], F32)
         for h in range(O_HALVES):
+            pass_words = w_words[:, h, g * PASS_WORDS : (g + 1) * PASS_WORDS].rearrange(
+                word_order, u=2
+            )
             for u in range(2):
-                first = (2 * g + u) * P
-                nc.tensor.transpose(bank[:, h, u, :], w_words[:, h, first : first + P], ident[:])
+                nc.tensor.transpose(bank[:, h, u, :], pass_words[:, u, :], ident[:])
         nc.scalar.copy(
             out=grouped_words[:, g].rearrange("p (h o) u -> p h o u", h=O_HALVES),
             in_=bank[:].rearrange("p h u o -> p h o u"),
@@ -104,8 +109,8 @@ def load_pts_chunk(nc, raw, pts_feat0, chunk):
     channels = slice(chunk * CHUNK_CH, (chunk + 1) * CHUNK_CH)
     for n in range(SAMPLES):
         nc.sync.dma_start(
-            out=pts_raw[:, n].rearrange("p (m e) s -> p m (e s)", e=2),
-            in_=pts_feat0[n, channels].rearrange("(m p e) h w -> p m (e h w)", p=P, e=2),
+            out=pts_raw[:, n].rearrange("p (g t) s -> p g (t s)", t=PACK),
+            in_=pts_feat0[n, channels].rearrange("(g p t) h w -> p g (t h w)", p=P, t=PACK),
         )
     return pts_raw
 
@@ -278,7 +283,7 @@ def tile_prefusioncat_k_kernel(
         img_w_scales = img.tile([P, PASSES, OUT_CH], U8, align_bytes=64)
         for chunk in range(CHUNKS):
             w_raw = load_weight_chunk(nc, w_in, img_w, chunk)
-            w_grouped = transpose_weight_chunk(nc, banks, work, ident, w_raw)
+            w_grouped = transpose_weight_chunk(nc, banks, work, ident, w_raw, WORDS_IN_HALVES)
             passes = slice(chunk * CHUNK_PASSES, (chunk + 1) * CHUNK_PASSES)
             quantise_chunk(nc, w_grouped, img_w_codes[:, passes], img_w_scales[:, passes])
 
@@ -366,7 +371,9 @@ def tile_prefusioncat_k_kernel(
             if chunk < CHUNKS:
                 w_raw = load_weight_chunk(nc, w_in, pts_w, chunk)
                 pts_raw = load_pts_chunk(nc, pts_in, pts_feat0, chunk)
-                w_grouped = transpose_weight_chunk(nc, banks, work, ident, w_raw)
+                w_grouped = transpose_weight_chunk(
+                    nc, banks, work, ident, w_raw, WORDS_ALTERNATING
+                )
                 pts_grouped = regroup_pts_chunk(nc, work, pts_raw)
                 w_codes = work.tile([P, CHUNK_PASSES, OUT_CH], U32, align_bytes=64)
                 w_scales = work.tile([P, CHUNK_PASSES, OUT_CH], U8, align_bytes=64)

@@ -118,12 +118,14 @@ def load_pts_chunk(nc, raw, pts_feat0, chunk):
 def regroup_pts_chunk(nc, work, pts_raw):
     pts_grouped = work.tile([P, CHUNK_PASSES, SAMPLES * POSITIONS, PACK], BF16, align_bytes=64)
     for n in range(SAMPLES):
-        nc.vector.tensor_copy(
-            out=pts_grouped[:, :, n * POSITIONS : (n + 1) * POSITIONS, :].rearrange(
-                "p g (c i) t -> p g c t i", i=4
-            ),
-            in_=pts_raw[:, n].rearrange("p (g t) (c i) -> p g c t i", t=PACK, i=4),
+        dst = pts_grouped[:, :, n * POSITIONS : (n + 1) * POSITIONS, :].rearrange(
+            "p g (c i) t -> p g c t i", i=4
         )
+        src = pts_raw[:, n].rearrange("p (g t) (c i) -> p g c t i", t=PACK, i=4)
+        vector_passes = CHUNK_PASSES if n < SAMPLES - 1 else CHUNK_PASSES // 2
+        nc.vector.tensor_copy(out=dst[:, 0:vector_passes], in_=src[:, 0:vector_passes])
+        for g in range(vector_passes, CHUNK_PASSES):
+            nc.scalar.copy(out=dst[:, g], in_=src[:, g])
     return pts_grouped
 
 
@@ -158,15 +160,16 @@ def tile_prefusioncat_k_kernel(
     out,
 ):
     nc = tc.nc
-    with ExitStack() as pools:
-        const = pools.enter_context(tc.tile_pool(name="const", bufs=1))
-        img = pools.enter_context(tc.tile_pool(name="img", bufs=1))
-        w_in = pools.enter_context(tc.tile_pool(name="w_in", bufs=4))
-        pts_in = pools.enter_context(tc.tile_pool(name="pts_in", bufs=3))
-        work = pools.enter_context(tc.tile_pool(name="work", bufs=2))
-        results = pools.enter_context(tc.tile_pool(name="results", bufs=2))
-        banks = pools.enter_context(tc.psum_pool(name="banks", bufs=5))
-        sums = pools.enter_context(tc.psum_pool(name="sums", bufs=1))
+    with ExitStack() as stack:
+        const = stack.enter_context(tc.tile_pool(name="const", bufs=1))
+        img = stack.enter_context(tc.tile_pool(name="img", bufs=1))
+        w_in = stack.enter_context(tc.tile_pool(name="w_in", bufs=4))
+        pts_in = stack.enter_context(tc.tile_pool(name="pts_in", bufs=2))
+        work = stack.enter_context(tc.tile_pool(name="work", bufs=2))
+        results = stack.enter_context(tc.tile_pool(name="results", bufs=2))
+        banks = stack.enter_context(tc.psum_pool(name="banks", bufs=5))
+        sums = stack.enter_context(tc.psum_pool(name="sums", bufs=1))
+        stack.enter_context(tc.manual_schedule())
 
         ident = const.tile([P, P], F32)
         make_identity(nc, ident[:])
@@ -185,105 +188,138 @@ def tile_prefusioncat_k_kernel(
                     in_=vectors[b][v].rearrange("(h o) -> h o", h=O_HALVES),
                 )
 
-        l1_raw = img.tile([P, RUN, L1_H * L1_W], BF16)
+        l3_rows = img.tile([P, RUN], BF16)
         nc.sync.dma_start(
-            out=l1_raw[:], in_=img_feat1.rearrange("n (m q) h w -> (n m) q (h w)", q=RUN)
+            out=l3_rows[:], in_=img_feat3.rearrange("n (m q) h w -> (n m) (q h w)", q=RUN)
         )
-        l2_raw = img.tile([P, RUN, L2_W], BF16)
+        l4_rows = img.tile([P, RUN], BF16)
         nc.sync.dma_start(
-            out=l2_raw[:], in_=img_feat2.rearrange("n (m q) h w -> (n m) q (h w)", q=RUN)
+            out=l4_rows[:], in_=img_feat4.rearrange("n (m q) h w -> (n m) (q h w)", q=RUN)
         )
-        l3_raw = img.tile([P, RUN], BF16)
+        l2_rows = img.tile([P, RUN, L2_W], BF16)
         nc.sync.dma_start(
-            out=l3_raw[:], in_=img_feat3.rearrange("n (m q) h w -> (n m) (q h w)", q=RUN)
+            out=l2_rows[:], in_=img_feat2.rearrange("n (m q) h w -> (n m) q (h w)", q=RUN)
         )
-        l4_raw = img.tile([P, RUN], BF16)
+        l1_rows = img.tile([P, RUN, L1_H * L1_W], BF16)
         nc.sync.dma_start(
-            out=l4_raw[:], in_=img_feat4.rearrange("n (m q) h w -> (n m) (q h w)", q=RUN)
+            out=l1_rows[:], in_=img_feat1.rearrange("n (m q) h w -> (n m) q (h w)", q=RUN)
         )
-        l0_raw = img.tile([P, SAMPLES, PASSES * PACK, GRID], BF16)
-        for n in range(SAMPLES):
-            nc.sync.dma_start(
-                out=l0_raw[:, n].rearrange("p (m e) s -> p m (e s)", e=2),
-                in_=img_feat0[n].rearrange("(m p e) h w -> p m (e h w)", p=P, e=2),
-            )
+        l0_rows = img.tile([P, RUN, GRID], BF16)
 
-        sum34 = img.tile([P, RUN], F32)
-        nc.vector.tensor_tensor(out=sum34[:], in0=l3_raw[:], in1=l4_raw[:], op=ADD)
-        sum234 = img.tile([P, RUN, L2_W], F32)
-        nc.vector.tensor_tensor(
-            out=sum234[:],
-            in0=l2_raw[:],
-            in1=sum34[:].unsqueeze(2).to_broadcast([P, RUN, L2_W]),
-            op=ADD,
-        )
         lower = img.tile([P, L1_H, L1_W, 2, P], F32)
-        l1_view = l1_raw[:].rearrange("p (x e) (r d k) -> p r e d k x", e=2, r=L1_H, d=L2_W)
-        sum234_view = sum234[:].rearrange("p (x e) d -> p e d x", e=2)
-        for r in range(L1_H):
-            for e in range(2):
-                nc.vector.tensor_tensor(
-                    out=lower[:, r, :, e, :].rearrange("p (d k) x -> p d k x", d=L2_W),
-                    in0=l1_view[:, r, e],
-                    in1=sum234_view[:, e].unsqueeze(2).to_broadcast([P, L2_W, L1_W // L2_W, P]),
-                    op=ADD,
-                )
         lower_t = img.tile([P, L1_H, L1_W, SAMPLES, PASSES, PACK], F32)
-        for r in range(L1_H):
-            for d in range(L2_W):
-                pair = slice(2 * d, 2 * d + 2)
-                lower_bank = banks.tile([P, 2, 2, P], F32, tag="bank")
-                for k in range(2):
-                    for e in range(2):
-                        nc.tensor.transpose(
-                            lower_bank[:, k, e, :], lower[:, r, 2 * d + k, e, :], ident[:]
-                        )
-                nc.scalar.copy(
-                    out=lower_t[:, r, pair].rearrange("p k n g (u e) -> p k (n g u) e", e=2),
-                    in_=lower_bank[:].rearrange("p k e q -> p k q e"),
-                )
-        img_grouped = img.tile([P, PASSES, SAMPLES * GRID, PACK], BF16, align_bytes=64)
-        l0_view = l0_raw[:].rearrange("p n (g t) s -> p n g s t", t=PACK)
-        for n in range(SAMPLES):
-            for i in range(GRID_H):
-                r = padded_source(GRID_TOP + i, TH, L1_H, n + 1)
-                for c in range(L1_W):
-                    cols = [
-                        j
-                        for j in range(GRID_W)
-                        if padded_source(GRID_LEFT + j, TW, L1_W, n + 1) == c
-                    ]
-                    first = i * GRID_W + cols[0]
-                    nc.vector.tensor_tensor(
-                        out=img_grouped[:, :, n * GRID + first : n * GRID + first + len(cols), :],
-                        in0=l0_view[:, n, :, first : first + len(cols), :],
-                        in1=lower_t[:, r, c, n]
-                        .unsqueeze(2)
-                        .to_broadcast([P, PASSES, len(cols), PACK]),
-                        op=ADD,
-                    )
+        l0_t = img.tile([P, SAMPLES, PASSES * PACK, GRID], BF16)
         img_cols = SAMPLES * GRID
+        img_grouped = img.tile([P, PASSES, img_cols, PACK], BF16, align_bytes=64)
         img_codes = img.tile([P, PASSES * img_cols + MIN_MOVING - img_cols], U32, align_bytes=64)
         img_scales = img.tile([P, PASSES * img_cols + MIN_MOVING - img_cols], U8, align_bytes=64)
         nc.vector.memset(img_codes[:, PASSES * img_cols :].bitcast(I32), 0)
         nc.vector.memset(img_scales[:, PASSES * img_cols :].bitcast(I32), 0)
-        half = PASSES // 2
-        for part in range(2):
-            nc.vector.quantize_mx(
-                out=img_codes[:, part * half * img_cols : (part + 1) * half * img_cols].bitcast(
-                    FP8X4
-                ),
-                scales=img_scales[:, part * half * img_cols : (part + 1) * half * img_cols],
-                in_=img_grouped[:, part * half : (part + 1) * half].rearrange(
-                    "p g c t -> p (g c t)"
-                ),
-            )
-
         img_w_codes = img.tile([P, PASSES, OUT_CH], U32, align_bytes=64)
         img_w_scales = img.tile([P, PASSES, OUT_CH], U8, align_bytes=64)
+
+        def add_lower_levels():
+            sum34 = img.tile([P, RUN], F32)
+            nc.vector.tensor_tensor(out=sum34[:], in0=l3_rows[:], in1=l4_rows[:], op=ADD)
+            sum234 = img.tile([P, RUN, L2_W], F32)
+            nc.vector.tensor_tensor(
+                out=sum234[:],
+                in0=l2_rows[:],
+                in1=sum34[:].unsqueeze(2).to_broadcast([P, RUN, L2_W]),
+                op=ADD,
+            )
+            l1_view = l1_rows[:].rearrange("p (x e) (r d k) -> p r e d k x", e=2, r=L1_H, d=L2_W)
+            sum234_view = sum234[:].rearrange("p (x e) d -> p e d x", e=2)
+            for r in range(L1_H):
+                for e in range(2):
+                    nc.vector.tensor_tensor(
+                        out=lower[:, r, :, e, :].rearrange("p (d k) x -> p d k x", d=L2_W),
+                        in0=l1_view[:, r, e],
+                        in1=sum234_view[:, e]
+                        .unsqueeze(2)
+                        .to_broadcast([P, L2_W, L1_W // L2_W, P]),
+                        op=ADD,
+                    )
+
+        def transpose_lower_levels():
+            for r in range(L1_H):
+                for d in range(L2_W):
+                    lower_bank = banks.tile([P, 2, 2, P], F32, tag="bank")
+                    for k in range(2):
+                        for e in range(2):
+                            nc.tensor.transpose(
+                                lower_bank[:, k, e, :], lower[:, r, 2 * d + k, e, :], ident[:]
+                            )
+                    nc.scalar.copy(
+                        out=lower_t[:, r, 2 * d : 2 * d + 2].rearrange(
+                            "p k n g (u e) -> p k (n g u) e", e=2
+                        ),
+                        in_=lower_bank[:].rearrange("p k e q -> p k q e"),
+                    )
+
+        def transpose_level0_row(i):
+            l0_words = l0_rows[:].bitcast(F32).rearrange("p (x e) (i k) -> p e i k x", e=2, i=GRID_H)
+            l0_t_words = l0_t[:].bitcast(F32).rearrange(
+                "p n (m e) (i k) -> p e i (n m) k", e=2, i=GRID_H
+            )
+            for e in range(2):
+                l0_bank = banks.tile([P, GRID_W // 2, P], F32, tag="bank")
+                for k in range(GRID_W // 2):
+                    nc.tensor.transpose(l0_bank[:, k, :], l0_words[:, e, i, k, :], ident[:])
+                nc.scalar.copy(
+                    out=l0_t_words[:, e, i], in_=l0_bank[:].rearrange("p k q -> p q k")
+                )
+
+        def add_grid_row(i):
+            l0_view = l0_t[:].rearrange("p n (g t) s -> p n g s t", t=PACK)
+            for n in range(SAMPLES):
+                r = padded_source(GRID_TOP + i, TH, L1_H, n + 1)
+                for j in range(0, GRID_W, 2):
+                    c0 = padded_source(GRID_LEFT + j, TW, L1_W, n + 1)
+                    c1 = padded_source(GRID_LEFT + j + 1, TW, L1_W, n + 1)
+                    if c0 == c1:
+                        lower_pair = (
+                            lower_t[:, r, c0, n].unsqueeze(2).to_broadcast([P, PASSES, 2, PACK])
+                        )
+                    else:
+                        assert c1 == c0 + 1
+                        lower_pair = lower_t[:, r, c0 : c1 + 1, n].rearrange("p c g t -> p g c t")
+                    first = i * GRID_W + j
+                    nc.vector.tensor_tensor(
+                        out=img_grouped[:, :, n * GRID + first : n * GRID + first + 2, :],
+                        in0=l0_view[:, n, :, first : first + 2, :],
+                        in1=lower_pair,
+                        op=ADD,
+                    )
+
+        def quantise_img_m():
+            half = PASSES // 2
+            for part in range(2):
+                cols = slice(part * half * img_cols, (part + 1) * half * img_cols)
+                nc.vector.quantize_mx(
+                    out=img_codes[:, cols].bitcast(FP8X4),
+                    scales=img_scales[:, cols],
+                    in_=img_grouped[:, part * half : (part + 1) * half].rearrange(
+                        "p g c t -> p (g c t)"
+                    ),
+                )
+
         for chunk in range(CHUNKS):
             w_raw = load_weight_chunk(nc, w_in, img_w, chunk)
+            if chunk == 0:
+                nc.sync.dma_start(
+                    out=l0_rows[:], in_=img_feat0.rearrange("n (m q) h w -> (n m) q (h w)", q=RUN)
+                )
             w_grouped = transpose_weight_chunk(nc, banks, work, ident, w_raw, WORDS_IN_HALVES)
+            if chunk == 0:
+                add_lower_levels()
+                transpose_lower_levels()
+            if chunk < GRID_H:
+                transpose_level0_row(chunk)
+            if 1 <= chunk <= GRID_H:
+                add_grid_row(chunk - 1)
+            if chunk == GRID_H + 1:
+                quantise_img_m()
             passes = slice(chunk * CHUNK_PASSES, (chunk + 1) * CHUNK_PASSES)
             quantise_chunk(nc, w_grouped, img_w_codes[:, passes], img_w_scales[:, passes])
 
@@ -312,91 +348,105 @@ def tile_prefusioncat_k_kernel(
         nc.vector.tensor_add(out=bn_shift[:], in0=scaled[:], in1=beta)
 
         img_sum = sums.tile([P, O_HALVES, MIN_MOVING], F32)
-        for h in range(O_HALVES):
-            o_cols = slice(h * P, (h + 1) * P)
-            for g in range(PASSES):
-                moving = slice(g * img_cols, g * img_cols + MIN_MOVING)
-                nc.tensor.matmul_mx(
-                    out=img_sum[:, h, :],
-                    lhsT=img_w_codes[:, g, o_cols].bitcast(FP8X4),
-                    lhsT_scale=img_w_scales[:, g, o_cols],
-                    rhs=img_codes[:, moving].bitcast(FP8X4),
-                    rhs_scale=img_scales[:, moving],
-                    start=(g == 0),
-                    stop=(g == PASSES - 1),
+
+        def multiply_img():
+            for h in range(O_HALVES):
+                o_cols = slice(h * P, (h + 1) * P)
+                for g in range(PASSES):
+                    moving = slice(g * img_cols, g * img_cols + MIN_MOVING)
+                    nc.tensor.matmul_mx(
+                        out=img_sum[:, h, :],
+                        lhsT=img_w_codes[:, g, o_cols].bitcast(FP8X4),
+                        lhsT_scale=img_w_scales[:, g, o_cols],
+                        rhs=img_codes[:, moving].bitcast(FP8X4),
+                        rhs_scale=img_scales[:, moving],
+                        start=(g == 0),
+                        stop=(g == PASSES - 1),
+                    )
+
+        def finish_img():
+            for h in range(O_HALVES):
+                grid = img_sum[:, h, 0:img_cols].rearrange(
+                    "p (n i j) -> p n i j", n=SAMPLES, i=GRID_H
                 )
-        for h in range(O_HALVES):
-            grid = img_sum[:, h, 0:img_cols].rearrange(
-                "p (n i j) -> p n i j", n=SAMPLES, i=GRID_H
-            )
-            img_res = results.tile([P, SAMPLES, TH, TW], F32)
-            rows = slice(GRID_TOP, GRID_TOP + GRID_H)
-            right = GRID_LEFT + GRID_W
-            for dst_cols, src in (
-                (slice(GRID_LEFT, right), grid),
-                (slice(0, GRID_LEFT), grid[:, :, :, 0:1]),
-                (slice(right, TW), grid[:, :, :, GRID_W - 1 : GRID_W]),
-            ):
-                dst = img_res[:, :, rows, dst_cols]
-                nc.scalar.activation(
-                    out=dst,
-                    in_=src.to_broadcast(dst.shape),
-                    func=RELU,
-                    bias=bn_shift[:, 0, h : h + 1],
-                    scale=bn_scale[:, 0, h : h + 1],
+                img_res = results.tile([P, SAMPLES, TH, TW], F32)
+                rows = slice(GRID_TOP, GRID_TOP + GRID_H)
+                right = GRID_LEFT + GRID_W
+                for dst_cols, src in (
+                    (slice(GRID_LEFT, right), grid),
+                    (slice(0, GRID_LEFT), grid[:, :, :, 0:1]),
+                    (slice(right, TW), grid[:, :, :, GRID_W - 1 : GRID_W]),
+                ):
+                    dst = img_res[:, :, rows, dst_cols]
+                    nc.scalar.activation(
+                        out=dst,
+                        in_=src.to_broadcast(dst.shape),
+                        func=RELU,
+                        bias=bn_shift[:, 0, h : h + 1],
+                        scale=bn_scale[:, 0, h : h + 1],
+                    )
+                nc.scalar.copy(
+                    out=img_res[:, :, 0:GRID_TOP, :],
+                    in_=img_res[:, :, GRID_TOP : GRID_TOP + 1, :].to_broadcast(
+                        [P, SAMPLES, GRID_TOP, TW]
+                    ),
                 )
-            nc.scalar.copy(
-                out=img_res[:, :, 0:GRID_TOP, :],
-                in_=img_res[:, :, GRID_TOP : GRID_TOP + 1, :].to_broadcast(
-                    [P, SAMPLES, GRID_TOP, TW]
-                ),
-            )
-            bottom = GRID_TOP + GRID_H
-            nc.scalar.copy(
-                out=img_res[:, :, bottom:TH, :],
-                in_=img_res[:, :, bottom - 1 : bottom, :].to_broadcast(
-                    [P, SAMPLES, TH - bottom, TW]
-                ),
-            )
-            nc.scalar.dma_start(
-                out=out[:, h * P : (h + 1) * P].rearrange("n o h w -> o n (h w)"),
-                in_=img_res[:].rearrange("p n h w -> p n (h w)"),
-            )
+                bottom = GRID_TOP + GRID_H
+                nc.scalar.copy(
+                    out=img_res[:, :, bottom:TH, :],
+                    in_=img_res[:, :, bottom - 1 : bottom, :].to_broadcast(
+                        [P, SAMPLES, TH - bottom, TW]
+                    ),
+                )
+                nc.scalar.dma_start(
+                    out=out[:, h * P : (h + 1) * P].rearrange("n o h w -> o n (h w)"),
+                    in_=img_res[:].rearrange("p n h w -> p n (h w)"),
+                )
 
         pts_sums = [
             sums.tile([P, SAMPLES * POSITIONS], F32, name="pts_sum%d" % h) for h in range(O_HALVES)
         ]
         operands = {}
-        for chunk in range(CHUNKS + 1):
-            if chunk < CHUNKS:
-                w_raw = load_weight_chunk(nc, w_in, pts_w, chunk)
-                pts_raw = load_pts_chunk(nc, pts_in, pts_feat0, chunk)
-                w_grouped = transpose_weight_chunk(
-                    nc, banks, work, ident, w_raw, WORDS_ALTERNATING
-                )
-                pts_grouped = regroup_pts_chunk(nc, work, pts_raw)
-                w_codes = work.tile([P, CHUNK_PASSES, OUT_CH], U32, align_bytes=64)
-                w_scales = work.tile([P, CHUNK_PASSES, OUT_CH], U8, align_bytes=64)
-                quantise_chunk(nc, w_grouped, w_codes[:], w_scales[:])
-                pts_codes = work.tile([P, CHUNK_PASSES, SAMPLES * POSITIONS], U32, align_bytes=64)
-                pts_scales = work.tile([P, CHUNK_PASSES, SAMPLES * POSITIONS], U8, align_bytes=64)
-                quantise_chunk(nc, pts_grouped, pts_codes[:], pts_scales[:])
-                operands[chunk] = (w_codes, w_scales, pts_codes, pts_scales)
-            if chunk > 0:
-                w_codes, w_scales, pts_codes, pts_scales = operands[chunk - 1]
-                for g in range(CHUNK_PASSES):
-                    done = (chunk - 1) * CHUNK_PASSES + g
-                    for h in range(O_HALVES):
-                        o_cols = slice(h * P, (h + 1) * P)
-                        nc.tensor.matmul_mx(
-                            out=pts_sums[h][:],
-                            lhsT=w_codes[:, g, o_cols].bitcast(FP8X4),
-                            lhsT_scale=w_scales[:, g, o_cols],
-                            rhs=pts_codes[:, g, :].bitcast(FP8X4),
-                            rhs_scale=pts_scales[:, g, :],
-                            start=(done == 0),
-                            stop=(done == PASSES - 1),
-                        )
+
+        def prepare_pts(chunk):
+            w_raw = load_weight_chunk(nc, w_in, pts_w, chunk)
+            pts_raw = load_pts_chunk(nc, pts_in, pts_feat0, chunk)
+            w_grouped = transpose_weight_chunk(nc, banks, work, ident, w_raw, WORDS_ALTERNATING)
+            pts_grouped = regroup_pts_chunk(nc, work, pts_raw)
+            w_codes = work.tile([P, CHUNK_PASSES, OUT_CH], U32, align_bytes=64)
+            w_scales = work.tile([P, CHUNK_PASSES, OUT_CH], U8, align_bytes=64)
+            quantise_chunk(nc, w_grouped, w_codes[:], w_scales[:])
+            pts_codes = work.tile([P, CHUNK_PASSES, SAMPLES * POSITIONS], U32, align_bytes=64)
+            pts_scales = work.tile([P, CHUNK_PASSES, SAMPLES * POSITIONS], U8, align_bytes=64)
+            quantise_chunk(nc, pts_grouped, pts_codes[:], pts_scales[:])
+            operands[chunk] = (w_codes, w_scales, pts_codes, pts_scales)
+
+        def multiply_pts(chunk):
+            w_codes, w_scales, pts_codes, pts_scales = operands[chunk]
+            for g in range(CHUNK_PASSES):
+                done = chunk * CHUNK_PASSES + g
+                for h in range(O_HALVES):
+                    o_cols = slice(h * P, (h + 1) * P)
+                    nc.tensor.matmul_mx(
+                        out=pts_sums[h][:],
+                        lhsT=w_codes[:, g, o_cols].bitcast(FP8X4),
+                        lhsT_scale=w_scales[:, g, o_cols],
+                        rhs=pts_codes[:, g, :].bitcast(FP8X4),
+                        rhs_scale=pts_scales[:, g, :],
+                        start=(done == 0),
+                        stop=(done == PASSES - 1),
+                    )
+
+        prepare_pts(0)
+        multiply_img()
+        prepare_pts(1)
+        multiply_pts(0)
+        finish_img()
+        for chunk in range(2, CHUNKS):
+            prepare_pts(chunk)
+            multiply_pts(chunk - 1)
+        multiply_pts(CHUNKS - 1)
+
         for h in range(O_HALVES):
             pts_res = results.tile([P, SAMPLES, POSITIONS], F32)
             nc.scalar.activation(

@@ -115,8 +115,8 @@ def load_pts_chunk(nc, raw, pts_feat0, chunk):
     return pts_raw
 
 
-def regroup_pts_chunk(nc, work, pts_raw):
-    pts_grouped = work.tile([P, CHUNK_PASSES, SAMPLES * POSITIONS, PACK], BF16, align_bytes=64)
+def regroup_pts_chunk(nc, single, pts_raw):
+    pts_grouped = single.tile([P, CHUNK_PASSES, SAMPLES * POSITIONS, PACK], BF16, align_bytes=64)
     for n in range(SAMPLES):
         dst = pts_grouped[:, :, n * POSITIONS : (n + 1) * POSITIONS, :].rearrange(
             "p g (c i) t -> p g c t i", i=4
@@ -164,8 +164,9 @@ def tile_prefusioncat_k_kernel(
         const = stack.enter_context(tc.tile_pool(name="const", bufs=1))
         img = stack.enter_context(tc.tile_pool(name="img", bufs=1))
         w_in = stack.enter_context(tc.tile_pool(name="w_in", bufs=4))
-        pts_in = stack.enter_context(tc.tile_pool(name="pts_in", bufs=2))
+        pts_in = stack.enter_context(tc.tile_pool(name="pts_in", bufs=3))
         work = stack.enter_context(tc.tile_pool(name="work", bufs=2))
+        single = stack.enter_context(tc.tile_pool(name="single", bufs=1))
         results = stack.enter_context(tc.tile_pool(name="results", bufs=2))
         banks = stack.enter_context(tc.psum_pool(name="banks", bufs=5))
         sums = stack.enter_context(tc.psum_pool(name="sums", bufs=1))
@@ -173,6 +174,11 @@ def tile_prefusioncat_k_kernel(
 
         ident = const.tile([P, P], F32)
         make_identity(nc, ident[:])
+
+        ones = const.tile([P, 1], F32)
+        nc.vector.memset(ones[:], 1.0)
+        table_warmer = const.tile([P, 1], F32)
+        nc.scalar.sqrt(out=table_warmer[:], in_=ones[:])
 
         vectors = (
             (img_b, img_gamma, img_beta, img_mean, img_var),
@@ -412,7 +418,7 @@ def tile_prefusioncat_k_kernel(
             w_raw = load_weight_chunk(nc, w_in, pts_w, chunk)
             pts_raw = load_pts_chunk(nc, pts_in, pts_feat0, chunk)
             w_grouped = transpose_weight_chunk(nc, banks, work, ident, w_raw, WORDS_ALTERNATING)
-            pts_grouped = regroup_pts_chunk(nc, work, pts_raw)
+            pts_grouped = regroup_pts_chunk(nc, single, pts_raw)
             w_codes = work.tile([P, CHUNK_PASSES, OUT_CH], U32, align_bytes=64)
             w_scales = work.tile([P, CHUNK_PASSES, OUT_CH], U8, align_bytes=64)
             quantise_chunk(nc, w_grouped, w_codes[:], w_scales[:])
@@ -456,7 +462,8 @@ def tile_prefusioncat_k_kernel(
                 bias=bn_shift[:, 1, h : h + 1],
                 scale=bn_scale[:, 1, h : h + 1],
             )
-            nc.sync.dma_start(
+            store_queue = nc.sync if h == 0 else nc.scalar
+            store_queue.dma_start(
                 out=out[:, OUT_CH + h * P : OUT_CH + (h + 1) * P].rearrange("n o h w -> o n (h w)"),
                 in_=pts_res[:],
             )

@@ -119,9 +119,9 @@ def regroup_pts_chunk(nc, single, pts_raw):
     pts_grouped = single.tile([P, CHUNK_PASSES, SAMPLES * POSITIONS, PACK], BF16, align_bytes=64)
     for n in range(SAMPLES):
         dst = pts_grouped[:, :, n * POSITIONS : (n + 1) * POSITIONS, :].rearrange(
-            "p g (c i) t -> p g c t i", i=4
+            "p g (c i) t -> p g c t i", i=2
         )
-        src = pts_raw[:, n].rearrange("p (g t) (c i) -> p g c t i", t=PACK, i=4)
+        src = pts_raw[:, n].rearrange("p (g t) (c i) -> p g c t i", t=PACK, i=2)
         vector_passes = CHUNK_PASSES if n < SAMPLES - 1 else CHUNK_PASSES // 2
         nc.vector.tensor_copy(out=dst[:, 0:vector_passes], in_=src[:, 0:vector_passes])
         for g in range(vector_passes, CHUNK_PASSES):

@@ -76,12 +76,19 @@ assert all(
 )
 
 
+def load_weights(nc, w_raw, w, chunk, passes):
+    first = chunk * CHUNK_CH
+    nc.sync.dma_start(
+        out=w_raw[:, :, passes.start * K_PASS : passes.stop * K_PASS],
+        in_=w[:, first + passes.start * K_PASS : first + passes.stop * K_PASS].rearrange(
+            "(h o) c -> o h c", h=O_HALVES
+        ),
+    )
+
+
 def load_weight_chunk(nc, raw, w, chunk):
     w_raw = raw.tile([P, O_HALVES, CHUNK_CH], BF16)
-    channels = slice(chunk * CHUNK_CH, (chunk + 1) * CHUNK_CH)
-    nc.sync.dma_start(
-        out=w_raw[:], in_=w[:, channels].rearrange("(h o) c -> o h c", h=O_HALVES)
-    )
+    load_weights(nc, w_raw, w, chunk, slice(0, CHUNK_PASSES))
     return w_raw
 
 
@@ -104,36 +111,39 @@ def transpose_weight_chunk(nc, banks, work, ident, w_raw, word_order):
     return w_grouped
 
 
-def load_pts_chunk(nc, raw, pts_feat0, chunk):
-    pts_raw = raw.tile([P, SAMPLES, CHUNK_PASSES * PACK, POSITIONS], BF16)
-    channels = slice(chunk * CHUNK_CH, (chunk + 1) * CHUNK_CH)
+def load_pts_passes(nc, pts_raw, pts_feat0, chunk, passes):
+    first = chunk * CHUNK_CH
     for n in range(SAMPLES):
         nc.sync.dma_start(
-            out=pts_raw[:, n].rearrange("p (g t) s -> p g (t s)", t=PACK),
-            in_=pts_feat0[n, channels].rearrange("(g p t) h w -> p g (t h w)", p=P, t=PACK),
+            out=pts_raw[:, n, passes.start * PACK : passes.stop * PACK].rearrange(
+                "p (g t) s -> p g (t s)", t=PACK
+            ),
+            in_=pts_feat0[
+                n, first + passes.start * K_PASS : first + passes.stop * K_PASS
+            ].rearrange("(g p t) h w -> p g (t h w)", p=P, t=PACK),
         )
-    return pts_raw
 
 
-def regroup_pts_chunk(nc, single, pts_raw):
-    pts_grouped = single.tile([P, CHUNK_PASSES, SAMPLES * POSITIONS, PACK], BF16, align_bytes=64)
+def regroup_pts_passes(nc, pts_grouped, pts_raw, passes):
     for n in range(SAMPLES):
         dst = pts_grouped[:, :, n * POSITIONS : (n + 1) * POSITIONS, :].rearrange(
             "p g (c i) t -> p g c t i", i=2
         )
         src = pts_raw[:, n].rearrange("p (g t) (c i) -> p g c t i", t=PACK, i=2)
-        vector_passes = CHUNK_PASSES if n < SAMPLES - 1 else CHUNK_PASSES // 2
-        nc.vector.tensor_copy(out=dst[:, 0:vector_passes], in_=src[:, 0:vector_passes])
-        for g in range(vector_passes, CHUNK_PASSES):
+        split = passes.stop if n < SAMPLES - 1 else (passes.start + passes.stop) // 2
+        if split > passes.start:
+            nc.vector.tensor_copy(
+                out=dst[:, passes.start : split], in_=src[:, passes.start : split]
+            )
+        for g in range(split, passes.stop):
             nc.scalar.copy(out=dst[:, g], in_=src[:, g])
-    return pts_grouped
 
 
 def quantise_chunk(nc, grouped, codes, scales):
     nc.vector.quantize_mx(
         out=codes.rearrange("p g c -> p (g c)").bitcast(FP8X4),
         scales=scales.rearrange("p g c -> p (g c)"),
-        in_=grouped[:].rearrange("p g c t -> p (g c t)"),
+        in_=grouped.rearrange("p g c t -> p (g c t)"),
     )
 
 
@@ -166,7 +176,8 @@ def tile_prefusioncat_k_kernel(
         w_in = stack.enter_context(tc.tile_pool(name="w_in", bufs=4))
         pts_in = stack.enter_context(tc.tile_pool(name="pts_in", bufs=3))
         work = stack.enter_context(tc.tile_pool(name="work", bufs=2))
-        single = stack.enter_context(tc.tile_pool(name="single", bufs=1))
+        coded = stack.enter_context(tc.tile_pool(name="coded", bufs=3))
+        single = stack.enter_context(tc.tile_pool(name="single", bufs=2))
         results = stack.enter_context(tc.tile_pool(name="results", bufs=2))
         banks = stack.enter_context(tc.psum_pool(name="banks", bufs=5))
         sums = stack.enter_context(tc.psum_pool(name="sums", bufs=1))
@@ -174,6 +185,11 @@ def tile_prefusioncat_k_kernel(
 
         ident = const.tile([P, P], F32)
         make_identity(nc, ident[:])
+        perm = const.tile([P, 2, SAMPLES, PASSES], F32)
+        nc.vector.tensor_copy(
+            out=perm[:], in_=ident[:].rearrange("p (n g u) -> p u n g", n=SAMPLES, u=2)
+        )
+        perm_halves = perm[:].rearrange("p u n g -> p u (n g)")
 
         ones = const.tile([P, 1], F32)
         nc.vector.memset(ones[:], 1.0)
@@ -194,6 +210,8 @@ def tile_prefusioncat_k_kernel(
                     in_=vectors[b][v].rearrange("(h o) -> h o", h=O_HALVES),
                 )
 
+        first_w_raw = w_in.tile([P, O_HALVES, CHUNK_CH], BF16, tag="w_raw")
+        load_weights(nc, first_w_raw, img_w, 0, slice(0, CHUNK_PASSES // 2))
         l3_rows = img.tile([P, RUN], BF16)
         nc.sync.dma_start(
             out=l3_rows[:], in_=img_feat3.rearrange("n (m q) h w -> (n m) (q h w)", q=RUN)
@@ -214,7 +232,6 @@ def tile_prefusioncat_k_kernel(
 
         lower = img.tile([P, L1_H, L1_W, 2, P], F32)
         lower_t = img.tile([P, L1_H, L1_W, SAMPLES, PASSES, PACK], F32)
-        l0_t = img.tile([P, SAMPLES, PASSES * PACK, GRID], BF16)
         img_cols = SAMPLES * GRID
         img_grouped = img.tile([P, PASSES, img_cols, PACK], BF16, align_bytes=64)
         img_codes = img.tile([P, PASSES * img_cols + MIN_MOVING - img_cols], U32, align_bytes=64)
@@ -263,26 +280,26 @@ def tile_prefusioncat_k_kernel(
                         in_=lower_bank[:].rearrange("p k e q -> p k q e"),
                     )
 
+        l0_banks = {}
+
         def transpose_level0_row(i):
             l0_words = l0_rows[:].bitcast(F32).rearrange("p (x e) (i k) -> p e i k x", e=2, i=GRID_H)
-            l0_t_words = l0_t[:].bitcast(F32).rearrange(
-                "p n (m e) (i k) -> p e i (n m) k", e=2, i=GRID_H
-            )
-            for e in range(2):
-                l0_bank = banks.tile([P, GRID_W // 2, P], F32, tag="bank")
-                for k in range(GRID_W // 2):
-                    nc.tensor.transpose(l0_bank[:, k, :], l0_words[:, e, i, k, :], ident[:])
-                nc.scalar.copy(
-                    out=l0_t_words[:, e, i], in_=l0_bank[:].rearrange("p k q -> p q k")
-                )
+            for quad in range(2):
+                bank = sums.tile([P, 2, 2, 2, SAMPLES * PASSES], F32, tag="pts_sum%d" % quad, name="l0_bank%d" % quad)
+                for k in range(2):
+                    for e in range(2):
+                        nc.tensor.transpose(
+                            bank[:, :, e, k, :], l0_words[:, e, i, 2 * quad + k, :], perm_halves
+                        )
+                l0_banks[i, quad] = bank
 
         def add_grid_row(i):
-            l0_view = l0_t[:].rearrange("p n (g t) s -> p n g s t", t=PACK)
-            for n in range(SAMPLES):
-                r = padded_source(GRID_TOP + i, TH, L1_H, n + 1)
-                for j in range(0, GRID_W, 2):
-                    c0 = padded_source(GRID_LEFT + j, TW, L1_W, n + 1)
-                    c1 = padded_source(GRID_LEFT + j + 1, TW, L1_W, n + 1)
+            for k in range(GRID_W // 2):
+                values = l0_banks[i, k // 2][:].bitcast(BF16)
+                for n in range(SAMPLES):
+                    r = padded_source(GRID_TOP + i, TH, L1_H, n + 1)
+                    c0 = padded_source(GRID_LEFT + 2 * k, TW, L1_W, n + 1)
+                    c1 = padded_source(GRID_LEFT + 2 * k + 1, TW, L1_W, n + 1)
                     if c0 == c1:
                         lower_pair = (
                             lower_t[:, r, c0, n].unsqueeze(2).to_broadcast([P, PASSES, 2, PACK])
@@ -290,10 +307,12 @@ def tile_prefusioncat_k_kernel(
                     else:
                         assert c1 == c0 + 1
                         lower_pair = lower_t[:, r, c0 : c1 + 1, n].rearrange("p c g t -> p g c t")
-                    first = i * GRID_W + j
+                    first = n * GRID + i * GRID_W + 2 * k
                     nc.vector.tensor_tensor(
-                        out=img_grouped[:, :, n * GRID + first : n * GRID + first + 2, :],
-                        in0=l0_view[:, n, :, first : first + 2, :],
+                        out=img_grouped[:, :, first : first + 2, :],
+                        in0=values[:, :, :, k % 2, n * 2 * PASSES : (n + 1) * 2 * PASSES].rearrange(
+                            "p u e (g s) -> p g s (u e)", s=2
+                        ),
                         in1=lower_pair,
                         op=ADD,
                     )
@@ -311,11 +330,14 @@ def tile_prefusioncat_k_kernel(
                 )
 
         for chunk in range(CHUNKS):
-            w_raw = load_weight_chunk(nc, w_in, img_w, chunk)
             if chunk == 0:
+                w_raw = first_w_raw
+                load_weights(nc, w_raw, img_w, 0, slice(CHUNK_PASSES // 2, CHUNK_PASSES))
                 nc.sync.dma_start(
                     out=l0_rows[:], in_=img_feat0.rearrange("n (m q) h w -> (n m) q (h w)", q=RUN)
                 )
+            else:
+                w_raw = load_weight_chunk(nc, w_in, img_w, chunk)
             w_grouped = transpose_weight_chunk(nc, banks, work, ident, w_raw, WORDS_IN_HALVES)
             if chunk == 0:
                 add_lower_levels()
@@ -327,38 +349,52 @@ def tile_prefusioncat_k_kernel(
             if chunk == GRID_H + 1:
                 quantise_img_m()
             passes = slice(chunk * CHUNK_PASSES, (chunk + 1) * CHUNK_PASSES)
-            quantise_chunk(nc, w_grouped, img_w_codes[:, passes], img_w_scales[:, passes])
+            quantise_chunk(nc, w_grouped[:], img_w_codes[:, passes], img_w_scales[:, passes])
 
-        vec_rows_f32 = const.tile([P, P], F32)
-        nc.vector.tensor_copy(out=vec_rows_f32[:], in_=vec_rows[:])
-        vec_bank = banks.tile([P, O_HALVES, 2, P], F32, tag="bank")
-        nc.tensor.transpose(vec_bank[:, 0, 0, :], vec_rows_f32[:], ident[:])
-        vec = const.tile([P, 2, 5, O_HALVES], F32)
-        nc.vector.tensor_copy(
-            out=vec[:].rearrange("p b v h -> p (b v h)"), in_=vec_bank[:, 0, 0, 0 : 2 * 5 * O_HALVES]
-        )
-        bias, gamma, beta, mean, var = (vec[:, :, v, :] for v in range(5))
-        var_eps = const.tile([P, 2, O_HALVES], F32)
-        nc.vector.tensor_scalar_add(out=var_eps[:], in0=var, scalar1=BN_EPS)
-        std = const.tile([P, 2, O_HALVES], F32)
-        nc.scalar.sqrt(out=std[:], in_=var_eps[:])
-        inv_std = const.tile([P, 2, O_HALVES], F32)
-        nc.vector.reciprocal(out=inv_std[:], in_=std[:])
-        bn_scale = const.tile([P, 2, O_HALVES], F32)
-        nc.vector.tensor_mul(out=bn_scale[:], in0=gamma, in1=inv_std[:])
-        centred = const.tile([P, 2, O_HALVES], F32)
-        nc.vector.tensor_sub(out=centred[:], in0=bias, in1=mean)
-        scaled = const.tile([P, 2, O_HALVES], F32)
-        nc.vector.tensor_mul(out=scaled[:], in0=centred[:], in1=bn_scale[:])
-        bn_shift = const.tile([P, 2, O_HALVES], F32)
-        nc.vector.tensor_add(out=bn_shift[:], in0=scaled[:], in1=beta)
+        bn = {}
+
+        def widen_vectors():
+            vec_rows_f32 = const.tile([P, P], F32)
+            nc.vector.tensor_copy(out=vec_rows_f32[:], in_=vec_rows[:])
+            bn["rows"] = vec_rows_f32
+
+        def transpose_vectors():
+            vec_bank = banks.tile([P, O_HALVES, 2, P], F32, tag="bank")
+            nc.tensor.transpose(vec_bank[:, 0, 0, :], bn["rows"][:], ident[:])
+            vec = const.tile([P, 2, 5, O_HALVES], F32)
+            nc.scalar.copy(
+                out=vec[:].rearrange("p b v h -> p (b v h)"),
+                in_=vec_bank[:, 0, 0, 0 : 2 * 5 * O_HALVES],
+            )
+            bn["vec"] = vec
+
+        def root_variance():
+            var_eps = const.tile([P, 2, O_HALVES], F32)
+            nc.vector.tensor_scalar_add(out=var_eps[:], in0=bn["vec"][:, :, 4, :], scalar1=BN_EPS)
+            std = const.tile([P, 2, O_HALVES], F32)
+            nc.scalar.sqrt(out=std[:], in_=var_eps[:])
+            bn["std"] = std
+
+        def fold_batch_norm():
+            bias, gamma, beta, mean = (bn["vec"][:, :, v, :] for v in range(4))
+            inv_std = const.tile([P, 2, O_HALVES], F32)
+            nc.vector.reciprocal(out=inv_std[:], in_=bn["std"][:])
+            bn_scale = const.tile([P, 2, O_HALVES], F32)
+            nc.vector.tensor_mul(out=bn_scale[:], in0=gamma, in1=inv_std[:])
+            centred = const.tile([P, 2, O_HALVES], F32)
+            nc.vector.tensor_sub(out=centred[:], in0=bias, in1=mean)
+            scaled = const.tile([P, 2, O_HALVES], F32)
+            nc.vector.tensor_mul(out=scaled[:], in0=centred[:], in1=bn_scale[:])
+            bn_shift = const.tile([P, 2, O_HALVES], F32)
+            nc.vector.tensor_add(out=bn_shift[:], in0=scaled[:], in1=beta)
+            bn["scale"], bn["shift"] = bn_scale, bn_shift
 
         img_sum = sums.tile([P, O_HALVES, MIN_MOVING], F32)
 
-        def multiply_img():
-            for h in range(O_HALVES):
-                o_cols = slice(h * P, (h + 1) * P)
-                for g in range(PASSES):
+        def multiply_img(h, part):
+            o_cols = slice(h * P, (h + 1) * P)
+            if True:
+                for g in range(part * PASSES // 2, (part + 1) * PASSES // 2):
                     moving = slice(g * img_cols, g * img_cols + MIN_MOVING)
                     nc.tensor.matmul_mx(
                         out=img_sum[:, h, :],
@@ -388,8 +424,8 @@ def tile_prefusioncat_k_kernel(
                         out=dst,
                         in_=src.to_broadcast(dst.shape),
                         func=RELU,
-                        bias=bn_shift[:, 0, h : h + 1],
-                        scale=bn_scale[:, 0, h : h + 1],
+                        bias=bn["shift"][:, 0, h : h + 1],
+                        scale=bn["scale"][:, 0, h : h + 1],
                     )
                 nc.scalar.copy(
                     out=img_res[:, :, 0:GRID_TOP, :],
@@ -410,21 +446,30 @@ def tile_prefusioncat_k_kernel(
                 )
 
         pts_sums = [
-            sums.tile([P, SAMPLES * POSITIONS], F32, name="pts_sum%d" % h) for h in range(O_HALVES)
+            sums.tile([P, SAMPLES * POSITIONS], F32, tag="pts_sum%d" % h, name="pts_sum%d" % h) for h in range(O_HALVES)
         ]
         operands = {}
 
-        def prepare_pts(chunk):
+        def prepare_pts(chunk, parts):
             w_raw = load_weight_chunk(nc, w_in, pts_w, chunk)
-            pts_raw = load_pts_chunk(nc, pts_in, pts_feat0, chunk)
+            pts_raw = pts_in.tile([P, SAMPLES, CHUNK_PASSES * PACK, POSITIONS], BF16)
+            for passes in parts:
+                load_pts_passes(nc, pts_raw, pts_feat0, chunk, passes)
             w_grouped = transpose_weight_chunk(nc, banks, work, ident, w_raw, WORDS_ALTERNATING)
-            pts_grouped = regroup_pts_chunk(nc, single, pts_raw)
-            w_codes = work.tile([P, CHUNK_PASSES, OUT_CH], U32, align_bytes=64)
-            w_scales = work.tile([P, CHUNK_PASSES, OUT_CH], U8, align_bytes=64)
-            quantise_chunk(nc, w_grouped, w_codes[:], w_scales[:])
-            pts_codes = work.tile([P, CHUNK_PASSES, SAMPLES * POSITIONS], U32, align_bytes=64)
-            pts_scales = work.tile([P, CHUNK_PASSES, SAMPLES * POSITIONS], U8, align_bytes=64)
-            quantise_chunk(nc, pts_grouped, pts_codes[:], pts_scales[:])
+            w_codes = coded.tile([P, CHUNK_PASSES, OUT_CH], U32, align_bytes=64)
+            w_scales = coded.tile([P, CHUNK_PASSES, OUT_CH], U8, align_bytes=64)
+            pts_grouped = single.tile(
+                [P, CHUNK_PASSES, SAMPLES * POSITIONS, PACK], BF16, align_bytes=64
+            )
+            pts_codes = coded.tile([P, CHUNK_PASSES, SAMPLES * POSITIONS], U32, align_bytes=64)
+            pts_scales = coded.tile([P, CHUNK_PASSES, SAMPLES * POSITIONS], U8, align_bytes=64)
+            for number, passes in enumerate(parts):
+                regroup_pts_passes(nc, pts_grouped, pts_raw, passes)
+                if number == 0:
+                    quantise_chunk(nc, w_grouped[:], w_codes[:], w_scales[:])
+                quantise_chunk(
+                    nc, pts_grouped[:, passes], pts_codes[:, passes], pts_scales[:, passes]
+                )
             operands[chunk] = (w_codes, w_scales, pts_codes, pts_scales)
 
         def multiply_pts(chunk):
@@ -443,14 +488,25 @@ def tile_prefusioncat_k_kernel(
                         stop=(done == PASSES - 1),
                     )
 
-        prepare_pts(0)
-        multiply_img()
-        prepare_pts(1)
-        multiply_pts(0)
-        finish_img()
-        for chunk in range(2, CHUNKS):
-            prepare_pts(chunk)
-            multiply_pts(chunk - 1)
+        whole = [slice(0, CHUNK_PASSES)]
+        last = [slice(0, 2), slice(2, 3), slice(3, 4)]
+        for chunk in range(CHUNKS):
+            prepare_pts(chunk, whole if chunk < CHUNKS - 1 else last)
+            if chunk == 0:
+                widen_vectors()
+            if chunk == 2:
+                transpose_vectors()
+            if chunk == 3:
+                root_variance()
+            if chunk == 4:
+                fold_batch_norm()
+            if 1 <= chunk <= 4:
+                multiply_img((chunk - 1) // 2, (chunk - 1) % 2)
+            if chunk >= 2:
+                multiply_pts(chunk - 2)
+            if chunk == 5:
+                finish_img()
+        multiply_pts(CHUNKS - 2)
         multiply_pts(CHUNKS - 1)
 
         for h in range(O_HALVES):
@@ -459,8 +515,8 @@ def tile_prefusioncat_k_kernel(
                 out=pts_res[:].rearrange("p n s -> p (n s)"),
                 in_=pts_sums[h][:],
                 func=RELU,
-                bias=bn_shift[:, 1, h : h + 1],
-                scale=bn_scale[:, 1, h : h + 1],
+                bias=bn["shift"][:, 1, h : h + 1],
+                scale=bn["scale"][:, 1, h : h + 1],
             )
             store_queue = nc.sync if h == 0 else nc.scalar
             store_queue.dma_start(

@@ -13,6 +13,14 @@ ADD = mybir.AluOpType.add
 RELU = mybir.ActivationFunctionType.Relu
 
 P = 128
+ITEMS = [("img", 0), ("img", 1)] + [
+    (branch, chunk + number) for chunk in range(1, 7) for number, branch in enumerate(("pts", "img"))
+] + [("pts", 7)]
+ROW = {0: (0, 0), 3: (1, 1), 6: (2, 2), 9: (3, 3)}
+ROW_T = {0: 0, 1: 1, 3: 2, 5: 3}
+ROW_A = {0: 0, 1: 1, 3: 2, 5: 3}
+QIMG = 7
+VSHARE = [4, 5, 5, 5, 5, 5, 5, 6]
 PACK = 4
 K_PASS = P * PACK
 
@@ -124,19 +132,19 @@ def load_pts_passes(nc, pts_raw, pts_feat0, chunk, passes):
         )
 
 
-def regroup_pts_passes(nc, pts_grouped, pts_raw, passes):
+def regroup_pts_passes(nc, pts_grouped, pts_raw, passes, extra):
     for n in range(SAMPLES):
         dst = pts_grouped[:, :, n * POSITIONS : (n + 1) * POSITIONS, :].rearrange(
             "p g (c i) t -> p g c t i", i=2
         )
         src = pts_raw[:, n].rearrange("p (g t) (c i) -> p g c t i", t=PACK, i=2)
-        split = passes.stop if n < SAMPLES - 1 else (passes.start + passes.stop) // 2
+        split = passes.stop if n < SAMPLES - 1 else passes.start + (passes.stop - passes.start) * (extra - 4) // 4
         if split > passes.start:
             nc.vector.tensor_copy(
                 out=dst[:, passes.start : split], in_=src[:, passes.start : split]
             )
-        for g in range(split, passes.stop):
-            nc.scalar.copy(out=dst[:, g], in_=src[:, g])
+        if split < passes.stop:
+            nc.scalar.copy(out=dst[:, split : passes.stop], in_=src[:, split : passes.stop])
 
 
 def quantise_chunk(nc, grouped, codes, scales):
@@ -175,11 +183,12 @@ def tile_prefusioncat_k_kernel(
         img = stack.enter_context(tc.tile_pool(name="img", bufs=1))
         w_in = stack.enter_context(tc.tile_pool(name="w_in", bufs=4))
         pts_in = stack.enter_context(tc.tile_pool(name="pts_in", bufs=3))
-        work = stack.enter_context(tc.tile_pool(name="work", bufs=2))
-        coded = stack.enter_context(tc.tile_pool(name="coded", bufs=3))
+        work = stack.enter_context(tc.tile_pool(name="work", bufs=3))
+        coded = stack.enter_context(tc.tile_pool(name="coded", bufs=2))
         single = stack.enter_context(tc.tile_pool(name="single", bufs=2))
         results = stack.enter_context(tc.tile_pool(name="results", bufs=2))
-        banks = stack.enter_context(tc.psum_pool(name="banks", bufs=5))
+        banks = stack.enter_context(tc.psum_pool(name="banks", bufs=4))
+        grids = stack.enter_context(tc.psum_pool(name="grids", bufs=1))
         sums = stack.enter_context(tc.psum_pool(name="sums", bufs=1))
         stack.enter_context(tc.manual_schedule())
 
@@ -210,8 +219,6 @@ def tile_prefusioncat_k_kernel(
                     in_=vectors[b][v].rearrange("(h o) -> h o", h=O_HALVES),
                 )
 
-        first_w_raw = w_in.tile([P, O_HALVES, CHUNK_CH], BF16, tag="w_raw")
-        load_weights(nc, first_w_raw, img_w, 0, slice(0, CHUNK_PASSES // 2))
         l3_rows = img.tile([P, RUN], BF16)
         nc.sync.dma_start(
             out=l3_rows[:], in_=img_feat3.rearrange("n (m q) h w -> (n m) (q h w)", q=RUN)
@@ -230,7 +237,7 @@ def tile_prefusioncat_k_kernel(
         )
         l0_rows = img.tile([P, RUN, GRID], BF16)
 
-        lower = img.tile([P, L1_H, L1_W, 2, P], F32)
+        lower = img.tile([P, RUN, L1_H, L1_W], F32)
         lower_t = img.tile([P, L1_H, L1_W, SAMPLES, PASSES, PACK], F32)
         img_cols = SAMPLES * GRID
         img_grouped = img.tile([P, PASSES, img_cols, PACK], BF16, align_bytes=64)
@@ -251,27 +258,24 @@ def tile_prefusioncat_k_kernel(
                 in1=sum34[:].unsqueeze(2).to_broadcast([P, RUN, L2_W]),
                 op=ADD,
             )
-            l1_view = l1_rows[:].rearrange("p (x e) (r d k) -> p r e d k x", e=2, r=L1_H, d=L2_W)
-            sum234_view = sum234[:].rearrange("p (x e) d -> p e d x", e=2)
+            l1_view = l1_rows[:].rearrange("p q (r d k) -> p q r d k", r=L1_H, d=L2_W)
             for r in range(L1_H):
-                for e in range(2):
-                    nc.vector.tensor_tensor(
-                        out=lower[:, r, :, e, :].rearrange("p (d k) x -> p d k x", d=L2_W),
-                        in0=l1_view[:, r, e],
-                        in1=sum234_view[:, e]
-                        .unsqueeze(2)
-                        .to_broadcast([P, L2_W, L1_W // L2_W, P]),
-                        op=ADD,
-                    )
+                nc.vector.tensor_tensor(
+                    out=lower[:, :, r].rearrange("p q (d k) -> p q d k", d=L2_W),
+                    in0=l1_view[:, :, r],
+                    in1=sum234[:].unsqueeze(3).to_broadcast([P, RUN, L2_W, L1_W // L2_W]),
+                    op=ADD,
+                )
 
         def transpose_lower_levels():
+            lower_words = lower[:].rearrange("p (x e) r c -> p r c e x", e=2)
             for r in range(L1_H):
                 for d in range(L2_W):
                     lower_bank = banks.tile([P, 2, 2, P], F32, tag="bank")
                     for k in range(2):
                         for e in range(2):
                             nc.tensor.transpose(
-                                lower_bank[:, k, e, :], lower[:, r, 2 * d + k, e, :], ident[:]
+                                lower_bank[:, k, e, :], lower_words[:, r, 2 * d + k, e, :], ident[:]
                             )
                     nc.scalar.copy(
                         out=lower_t[:, r, 2 * d : 2 * d + 2].rearrange(
@@ -285,7 +289,7 @@ def tile_prefusioncat_k_kernel(
         def transpose_level0_row(i):
             l0_words = l0_rows[:].bitcast(F32).rearrange("p (x e) (i k) -> p e i k x", e=2, i=GRID_H)
             for quad in range(2):
-                bank = sums.tile([P, 2, 2, 2, SAMPLES * PASSES], F32, tag="pts_sum%d" % quad, name="l0_bank%d" % quad)
+                bank = grids.tile([P, 2, 2, 2, SAMPLES * PASSES], F32, tag="img_sum%d" % quad, name="l0_bank%d" % quad)
                 for k in range(2):
                     for e in range(2):
                         nc.tensor.transpose(
@@ -329,25 +333,11 @@ def tile_prefusioncat_k_kernel(
                     ),
                 )
 
-        for chunk in range(CHUNKS):
-            if chunk == 0:
-                w_raw = first_w_raw
-                load_weights(nc, w_raw, img_w, 0, slice(CHUNK_PASSES // 2, CHUNK_PASSES))
-                nc.sync.dma_start(
-                    out=l0_rows[:], in_=img_feat0.rearrange("n (m q) h w -> (n m) q (h w)", q=RUN)
-                )
-            else:
-                w_raw = load_weight_chunk(nc, w_in, img_w, chunk)
+        def prepare_img(chunk):
+            w_raw = load_weight_chunk(nc, w_in, img_w, chunk)
+            if chunk == CHUNKS - 1:
+                raw[7] = load_weight_chunk(nc, w_in, pts_w, 7)
             w_grouped = transpose_weight_chunk(nc, banks, work, ident, w_raw, WORDS_IN_HALVES)
-            if chunk == 0:
-                add_lower_levels()
-                transpose_lower_levels()
-            if chunk < GRID_H:
-                transpose_level0_row(chunk)
-            if 1 <= chunk <= GRID_H:
-                add_grid_row(chunk - 1)
-            if chunk == GRID_H + 1:
-                quantise_img_m()
             passes = slice(chunk * CHUNK_PASSES, (chunk + 1) * CHUNK_PASSES)
             quantise_chunk(nc, w_grouped[:], img_w_codes[:, passes], img_w_scales[:, passes])
 
@@ -368,11 +358,14 @@ def tile_prefusioncat_k_kernel(
             )
             bn["vec"] = vec
 
-        def root_variance():
+        def raise_variance():
             var_eps = const.tile([P, 2, O_HALVES], F32)
             nc.vector.tensor_scalar_add(out=var_eps[:], in0=bn["vec"][:, :, 4, :], scalar1=BN_EPS)
+            bn["var_eps"] = var_eps
+
+        def take_root():
             std = const.tile([P, 2, O_HALVES], F32)
-            nc.scalar.sqrt(out=std[:], in_=var_eps[:])
+            nc.scalar.sqrt(out=std[:], in_=bn["var_eps"][:])
             bn["std"] = std
 
         def fold_batch_norm():
@@ -389,15 +382,15 @@ def tile_prefusioncat_k_kernel(
             nc.vector.tensor_add(out=bn_shift[:], in0=scaled[:], in1=beta)
             bn["scale"], bn["shift"] = bn_scale, bn_shift
 
-        img_sum = sums.tile([P, O_HALVES, MIN_MOVING], F32)
+        img_sums = []
 
-        def multiply_img(h, part):
-            o_cols = slice(h * P, (h + 1) * P)
-            if True:
-                for g in range(part * PASSES // 2, (part + 1) * PASSES // 2):
+        def multiply_img(chunk):
+            for h in range(O_HALVES):
+                o_cols = slice(h * P, (h + 1) * P)
+                for g in range(chunk * CHUNK_PASSES, (chunk + 1) * CHUNK_PASSES):
                     moving = slice(g * img_cols, g * img_cols + MIN_MOVING)
                     nc.tensor.matmul_mx(
-                        out=img_sum[:, h, :],
+                        out=img_sums[h][:],
                         lhsT=img_w_codes[:, g, o_cols].bitcast(FP8X4),
                         lhsT_scale=img_w_scales[:, g, o_cols],
                         rhs=img_codes[:, moving].bitcast(FP8X4),
@@ -406,9 +399,11 @@ def tile_prefusioncat_k_kernel(
                         stop=(g == PASSES - 1),
                     )
 
+        img_results = []
+
         def finish_img():
             for h in range(O_HALVES):
-                grid = img_sum[:, h, 0:img_cols].rearrange(
+                grid = img_sums[h][:, 0:img_cols].rearrange(
                     "p (n i j) -> p n i j", n=SAMPLES, i=GRID_H
                 )
                 img_res = results.tile([P, SAMPLES, TH, TW], F32)
@@ -440,18 +435,24 @@ def tile_prefusioncat_k_kernel(
                         [P, SAMPLES, TH - bottom, TW]
                     ),
                 )
-                nc.scalar.dma_start(
+                img_results.append(img_res)
+
+        def store_img():
+            for h in range(O_HALVES):
+                nc.sync.dma_start(
                     out=out[:, h * P : (h + 1) * P].rearrange("n o h w -> o n (h w)"),
-                    in_=img_res[:].rearrange("p n h w -> p n (h w)"),
+                    in_=img_results[h][:].rearrange("p n h w -> p n (h w)"),
                 )
 
         pts_sums = [
-            sums.tile([P, SAMPLES * POSITIONS], F32, tag="pts_sum%d" % h, name="pts_sum%d" % h) for h in range(O_HALVES)
+            sums.tile([P, SAMPLES * POSITIONS], F32, name="pts_sum%d" % h) for h in range(O_HALVES)
         ]
         operands = {}
 
+        raw = {}
+
         def prepare_pts(chunk, parts):
-            w_raw = load_weight_chunk(nc, w_in, pts_w, chunk)
+            w_raw = raw[chunk] if chunk in raw else load_weight_chunk(nc, w_in, pts_w, chunk)
             pts_raw = pts_in.tile([P, SAMPLES, CHUNK_PASSES * PACK, POSITIONS], BF16)
             for passes in parts:
                 load_pts_passes(nc, pts_raw, pts_feat0, chunk, passes)
@@ -464,7 +465,7 @@ def tile_prefusioncat_k_kernel(
             pts_codes = coded.tile([P, CHUNK_PASSES, SAMPLES * POSITIONS], U32, align_bytes=64)
             pts_scales = coded.tile([P, CHUNK_PASSES, SAMPLES * POSITIONS], U8, align_bytes=64)
             for number, passes in enumerate(parts):
-                regroup_pts_passes(nc, pts_grouped, pts_raw, passes)
+                regroup_pts_passes(nc, pts_grouped, pts_raw, passes, VSHARE[chunk])
                 if number == 0:
                     quantise_chunk(nc, w_grouped[:], w_codes[:], w_scales[:])
                 quantise_chunk(
@@ -490,23 +491,50 @@ def tile_prefusioncat_k_kernel(
 
         whole = [slice(0, CHUNK_PASSES)]
         last = [slice(0, 2), slice(2, 3), slice(3, 4)]
-        for chunk in range(CHUNKS):
-            prepare_pts(chunk, whole if chunk < CHUNKS - 1 else last)
-            if chunk == 0:
+        raw[0] = load_weight_chunk(nc, w_in, pts_w, 0)
+        add_lower_levels()
+        prepare_pts(0, whole)
+        transpose_lower_levels()
+        nc.sync.dma_start(
+            out=l0_rows[:], in_=img_feat0.rearrange("n (m q) h w -> (n m) q (h w)", q=RUN)
+        )
+        done_img = 0
+        for number, (branch, chunk) in enumerate(ITEMS):
+            if number in ROW_T:
+                transpose_level0_row(ROW_T[number])
+            if number in ROW_A:
+                add_grid_row(ROW_A[number])
+            if branch == "img":
+                prepare_img(chunk)
+            else:
+                prepare_pts(chunk, whole if chunk < CHUNKS - 1 else last)
+            if number == QIMG:
+                quantise_img_m()
+                img_sums += [
+                    grids.tile([P, MIN_MOVING], F32, tag="img_sum%d" % h, name="img_sum%d" % h)
+                    for h in range(O_HALVES)
+                ]
+            if number == 7:
                 widen_vectors()
-            if chunk == 2:
+            if number == 9:
                 transpose_vectors()
-            if chunk == 3:
-                root_variance()
-            if chunk == 4:
+            if number == 10:
+                raise_variance()
+            if number == 11:
+                take_root()
+            if number == 12:
                 fold_batch_norm()
-            if 1 <= chunk <= 4:
-                multiply_img((chunk - 1) // 2, (chunk - 1) % 2)
-            if chunk >= 2:
-                multiply_pts(chunk - 2)
-            if chunk == 5:
-                finish_img()
-        multiply_pts(CHUNKS - 2)
+            if number == 1:
+                multiply_pts(0)
+            elif number >= 2 and ITEMS[number - 2][0] == "pts":
+                multiply_pts(ITEMS[number - 2][1])
+            if number in (12, 13, 14):
+                for c in ((0, 1), (2, 3), (4, 5, 6))[number - 12]:
+                    multiply_img(c)
+        store_late = True
+        multiply_img(7)
+        finish_img()
+        store_img()
         multiply_pts(CHUNKS - 1)
 
         for h in range(O_HALVES):

@@ -19,6 +19,7 @@ ITEMS = [("img", 0), ("img", 1)] + [
 ROW = {0: (0, 0), 3: (1, 1), 6: (2, 2), 9: (3, 3)}
 ROW_T = {0: 0, 1: 1, 3: 2, 5: 3}
 ROW_A = {0: 0, 1: 1, 3: 2, 5: 3}
+MIMG = {9: (0,), 10: (1,), 11: (2, 3), 12: (4,), 13: (5,), 14: (6,)}
 QIMG = 7
 VSHARE = [4, 5, 5, 5, 5, 5, 5, 6]
 PACK = 4
@@ -195,7 +196,7 @@ def tile_prefusioncat_k_kernel(
         ident = const.tile([P, P], F32)
         make_identity(nc, ident[:])
         perm = const.tile([P, 2, SAMPLES, PASSES], F32)
-        nc.vector.tensor_copy(
+        nc.gpsimd.tensor_copy(
             out=perm[:], in_=ident[:].rearrange("p (n g u) -> p u n g", n=SAMPLES, u=2)
         )
         perm_halves = perm[:].rearrange("p u n g -> p u (n g)")
@@ -210,7 +211,7 @@ def tile_prefusioncat_k_kernel(
             (pts_b, pts_gamma, pts_beta, pts_mean, pts_var),
         )
         vec_rows = const.tile([P, P], BF16)
-        nc.vector.memset(vec_rows[:], 0.0)
+        nc.gpsimd.memset(vec_rows[:], 0.0)
         for b in range(2):
             for v in range(5):
                 row = (b * 5 + v) * O_HALVES
@@ -243,8 +244,8 @@ def tile_prefusioncat_k_kernel(
         img_grouped = img.tile([P, PASSES, img_cols, PACK], BF16, align_bytes=64)
         img_codes = img.tile([P, PASSES * img_cols + MIN_MOVING - img_cols], U32, align_bytes=64)
         img_scales = img.tile([P, PASSES * img_cols + MIN_MOVING - img_cols], U8, align_bytes=64)
-        nc.vector.memset(img_codes[:, PASSES * img_cols :].bitcast(I32), 0)
-        nc.vector.memset(img_scales[:, PASSES * img_cols :].bitcast(I32), 0)
+        nc.gpsimd.memset(img_codes[:, PASSES * img_cols :].bitcast(I32), 0)
+        nc.gpsimd.memset(img_scales[:, PASSES * img_cols :].bitcast(I32), 0)
         img_w_codes = img.tile([P, PASSES, OUT_CH], U32, align_bytes=64)
         img_w_scales = img.tile([P, PASSES, OUT_CH], U8, align_bytes=64)
 
@@ -306,16 +307,16 @@ def tile_prefusioncat_k_kernel(
                     c1 = padded_source(GRID_LEFT + 2 * k + 1, TW, L1_W, n + 1)
                     if c0 == c1:
                         lower_pair = (
-                            lower_t[:, r, c0, n].unsqueeze(2).to_broadcast([P, PASSES, 2, PACK])
+                            lower_t[:, r, c0, n].unsqueeze(3).to_broadcast([P, PASSES, PACK, 2])
                         )
                     else:
                         assert c1 == c0 + 1
-                        lower_pair = lower_t[:, r, c0 : c1 + 1, n].rearrange("p c g t -> p g c t")
+                        lower_pair = lower_t[:, r, c0 : c1 + 1, n].rearrange("p c g t -> p g t c")
                     first = n * GRID + i * GRID_W + 2 * k
                     nc.vector.tensor_tensor(
-                        out=img_grouped[:, :, first : first + 2, :],
+                        out=img_grouped[:, :, first : first + 2, :].rearrange("p g s t -> p g t s"),
                         in0=values[:, :, :, k % 2, n * 2 * PASSES : (n + 1) * 2 * PASSES].rearrange(
-                            "p u e (g s) -> p g s (u e)", s=2
+                            "p u e (g s) -> p g (u e) s", s=2
                         ),
                         in1=lower_pair,
                         op=ADD,
@@ -345,7 +346,7 @@ def tile_prefusioncat_k_kernel(
 
         def widen_vectors():
             vec_rows_f32 = const.tile([P, P], F32)
-            nc.vector.tensor_copy(out=vec_rows_f32[:], in_=vec_rows[:])
+            nc.gpsimd.tensor_copy(out=vec_rows_f32[:], in_=vec_rows[:])
             bn["rows"] = vec_rows_f32
 
         def transpose_vectors():
@@ -360,7 +361,7 @@ def tile_prefusioncat_k_kernel(
 
         def raise_variance():
             var_eps = const.tile([P, 2, O_HALVES], F32)
-            nc.vector.tensor_scalar_add(out=var_eps[:], in0=bn["vec"][:, :, 4, :], scalar1=BN_EPS)
+            nc.gpsimd.tensor_scalar_add(out=var_eps[:], in0=bn["vec"][:, :, 4, :], scalar1=BN_EPS)
             bn["var_eps"] = var_eps
 
         def take_root():
@@ -373,13 +374,13 @@ def tile_prefusioncat_k_kernel(
             inv_std = const.tile([P, 2, O_HALVES], F32)
             nc.vector.reciprocal(out=inv_std[:], in_=bn["std"][:])
             bn_scale = const.tile([P, 2, O_HALVES], F32)
-            nc.vector.tensor_mul(out=bn_scale[:], in0=gamma, in1=inv_std[:])
+            nc.gpsimd.tensor_mul(out=bn_scale[:], in0=gamma, in1=inv_std[:])
             centred = const.tile([P, 2, O_HALVES], F32)
-            nc.vector.tensor_sub(out=centred[:], in0=bias, in1=mean)
+            nc.gpsimd.tensor_sub(out=centred[:], in0=bias, in1=mean)
             scaled = const.tile([P, 2, O_HALVES], F32)
-            nc.vector.tensor_mul(out=scaled[:], in0=centred[:], in1=bn_scale[:])
+            nc.gpsimd.tensor_mul(out=scaled[:], in0=centred[:], in1=bn_scale[:])
             bn_shift = const.tile([P, 2, O_HALVES], F32)
-            nc.vector.tensor_add(out=bn_shift[:], in0=scaled[:], in1=beta)
+            nc.gpsimd.tensor_add(out=bn_shift[:], in0=scaled[:], in1=beta)
             bn["scale"], bn["shift"] = bn_scale, bn_shift
 
         img_sums = []
@@ -473,9 +474,9 @@ def tile_prefusioncat_k_kernel(
                 )
             operands[chunk] = (w_codes, w_scales, pts_codes, pts_scales)
 
-        def multiply_pts(chunk):
+        def multiply_pts(chunk, passes=slice(0, CHUNK_PASSES)):
             w_codes, w_scales, pts_codes, pts_scales = operands[chunk]
-            for g in range(CHUNK_PASSES):
+            for g in range(passes.start, passes.stop):
                 done = chunk * CHUNK_PASSES + g
                 for h in range(O_HALVES):
                     o_cols = slice(h * P, (h + 1) * P)
@@ -524,14 +525,14 @@ def tile_prefusioncat_k_kernel(
                 take_root()
             if number == 12:
                 fold_batch_norm()
-            if number == 1:
-                multiply_pts(0)
-            elif number >= 2 and ITEMS[number - 2][0] == "pts":
-                multiply_pts(ITEMS[number - 2][1])
-            if number in (12, 13, 14):
-                for c in ((0, 1), (2, 3), (4, 5, 6))[number - 12]:
-                    multiply_img(c)
-        store_late = True
+            if number in (1, 2):
+                multiply_pts(0, slice(2 * number - 2, 2 * number))
+            if number >= 4:
+                back = 2 if ITEMS[number - 2][0] == "pts" else 3
+                multiply_pts(ITEMS[number - back][1], slice(2 * back - 4, 2 * back - 2))
+            for c in MIMG.get(number, ()):
+                multiply_img(c)
+        multiply_pts(CHUNKS - 2, slice(2, 4))
         multiply_img(7)
         finish_img()
         store_img()

from contextlib import ExitStack

import concourse.mybir as mybir
from concourse.masks import make_identity

BF16 = mybir.dt.bfloat16
F32 = mybir.dt.float32
I32 = mybir.dt.int32
U32 = mybir.dt.uint32
U8 = mybir.dt.uint8
FP8X4 = mybir.dt.float8_e4m3fn_x4
ADD = mybir.AluOpType.add
RELU = mybir.ActivationFunctionType.Relu

P = 128
ITEMS = [("img", 0), ("img", 1)] + [
    (branch, chunk + number) for chunk in range(1, 7) for number, branch in enumerate(("pts", "img"))
] + [("pts", 7)]
ROW = {0: (0, 0), 3: (1, 1), 6: (2, 2), 9: (3, 3)}
ROW_T = {0: 0, 1: 1, 3: 2, 5: 3}
ROW_A = {0: 0, 1: 1, 3: 2, 5: 3}
MIMG = {9: (0,), 10: (1,), 11: (2, 3), 12: (4,), 13: (5,), 14: (6,)}
QIMG = 7
VSHARE = [4, 5, 5, 5, 5, 5, 5, 6]
PACK = 4
K_PASS = P * PACK

SAMPLES = 2
CHANNELS = 16384
OUT_CH = 256
O_HALVES = OUT_CH // P
TH, TW = 8, 16
POSITIONS = TH * TW
GRID_H, GRID_W = 4, 8
GRID_TOP, GRID_LEFT = (TH - GRID_H) // 2, (TW - GRID_W) // 2
GRID = GRID_H * GRID_W
L1_H, L1_W = 2, 4
L2_W = 2
BN_EPS = 1e-5

PASSES = CHANNELS // K_PASS
CHUNK_PASSES = 4
CHUNK_CH = CHUNK_PASSES * K_PASS
CHUNKS = PASSES // CHUNK_PASSES
PASS_WORDS = K_PASS // 2
RUN = 2 * P

MIN_MOVING = 128

WORDS_IN_HALVES = "o (u p) -> o u p"
WORDS_ALTERNATING = "o (p u) -> o u p"

FLOPS = 2 * 2 * OUT_CH * CHANNELS * SAMPLES * POSITIONS


def padded_source(index, size, level_size, repeat):
    length = level_size * repeat
    before = (size - length) // 2
    return min(max(index - before, 0), length - 1) // repeat


def grid_row(h):
    return min(max(h, GRID_TOP), GRID_TOP + GRID_H - 1)


def grid_col(w):
    return min(max(w, GRID_LEFT), GRID_LEFT + GRID_W - 1)


assert all(
    padded_source(h, TH, L1_H, rep) == padded_source(grid_row(h), TH, L1_H, rep)
    for rep in (1, 2)
    for h in range(TH)
)
assert all(
    padded_source(w, TW, size, rep) == padded_source(grid_col(w), TW, size, rep)
    for rep in (1, 2)
    for size in (L1_W, L2_W)
    for w in range(TW)
)
assert all(
    padded_source(w, TW, L2_W, rep) == padded_source(w, TW, L1_W, rep) // 2
    for rep in (1, 2)
    for w in range(TW)
)


def load_weights(nc, w_raw, w, chunk, passes):
    first = chunk * CHUNK_CH
    nc.sync.dma_start(
        out=w_raw[:, :, passes.start * K_PASS : passes.stop * K_PASS],
        in_=w[:, first + passes.start * K_PASS : first + passes.stop * K_PASS].rearrange(
            "(h o) c -> o h c", h=O_HALVES
        ),
    )


def load_weight_chunk(nc, raw, w, chunk):
    w_raw = raw.tile([P, O_HALVES, CHUNK_CH], BF16)
    load_weights(nc, w_raw, w, chunk, slice(0, CHUNK_PASSES))
    return w_raw


def transpose_weight_chunk(nc, banks, work, ident, w_raw, word_order):
    w_words = w_raw[:].bitcast(F32)
    w_grouped = work.tile([P, CHUNK_PASSES, OUT_CH, PACK], BF16, align_bytes=64)
    grouped_words = w_grouped[:].bitcast(F32)
    for g in range(CHUNK_PASSES):
        bank = banks.tile([P, O_HALVES, 2, P], F32)
        for h in range(O_HALVES):
            pass_words = w_words[:, h, g * PASS_WORDS : (g + 1) * PASS_WORDS].rearrange(
                word_order, u=2
            )
            for u in range(2):
                nc.tensor.transpose(bank[:, h, u, :], pass_words[:, u, :], ident[:])
        nc.scalar.copy(
            out=grouped_words[:, g].rearrange("p (h o) u -> p h o u", h=O_HALVES),
            in_=bank[:].rearrange("p h u o -> p h o u"),
        )
    return w_grouped


def load_pts_passes(nc, pts_raw, pts_feat0, chunk, passes):
    first = chunk * CHUNK_CH
    for n in range(SAMPLES):
        nc.sync.dma_start(
            out=pts_raw[:, n, passes.start * PACK : passes.stop * PACK].rearrange(
                "p (g t) s -> p g (t s)", t=PACK
            ),
            in_=pts_feat0[
                n, first + passes.start * K_PASS : first + passes.stop * K_PASS
            ].rearrange("(g p t) h w -> p g (t h w)", p=P, t=PACK),
        )


def regroup_pts_passes(nc, pts_grouped, pts_raw, passes, extra):
    for n in range(SAMPLES):
        dst = pts_grouped[:, :, n * POSITIONS : (n + 1) * POSITIONS, :].rearrange(
            "p g (c i) t -> p g c t i", i=2
        )
        src = pts_raw[:, n].rearrange("p (g t) (c i) -> p g c t i", t=PACK, i=2)
        split = passes.stop if n < SAMPLES - 1 else passes.start + (passes.stop - passes.start) * (extra - 4) // 4
        if split > passes.start:
            nc.vector.tensor_copy(
                out=dst[:, passes.start : split], in_=src[:, passes.start : split]
            )
        if split < passes.stop:
            nc.scalar.copy(out=dst[:, split : passes.stop], in_=src[:, split : passes.stop])


def quantise_chunk(nc, grouped, codes, scales):
    nc.vector.quantize_mx(
        out=codes.rearrange("p g c -> p (g c)").bitcast(FP8X4),
        scales=scales.rearrange("p g c -> p (g c)"),
        in_=grouped.rearrange("p g c t -> p (g c t)"),
    )


def tile_prefusioncat_k_kernel(
    tc,
    img_feat0,
    img_feat1,
    img_feat2,
    img_feat3,
    img_feat4,
    pts_feat0,
    img_w,
    img_b,
    img_gamma,
    img_beta,
    img_mean,
    img_var,
    pts_w,
    pts_b,
    pts_gamma,
    pts_beta,
    pts_mean,
    pts_var,
    out,
):
    nc = tc.nc
    with ExitStack() as stack:
        const = stack.enter_context(tc.tile_pool(name="const", bufs=1))
        img = stack.enter_context(tc.tile_pool(name="img", bufs=1))
        w_in = stack.enter_context(tc.tile_pool(name="w_in", bufs=4))
        pts_in = stack.enter_context(tc.tile_pool(name="pts_in", bufs=3))
        work = stack.enter_context(tc.tile_pool(name="work", bufs=3))
        coded = stack.enter_context(tc.tile_pool(name="coded", bufs=2))
        single = stack.enter_context(tc.tile_pool(name="single", bufs=2))
        results = stack.enter_context(tc.tile_pool(name="results", bufs=2))
        banks = stack.enter_context(tc.psum_pool(name="banks", bufs=4))
        grids = stack.enter_context(tc.psum_pool(name="grids", bufs=1))
        sums = stack.enter_context(tc.psum_pool(name="sums", bufs=1))
        stack.enter_context(tc.manual_schedule())

        ident = const.tile([P, P], F32)
        make_identity(nc, ident[:])
        perm = const.tile([P, 2, SAMPLES, PASSES], F32)
        nc.gpsimd.tensor_copy(
            out=perm[:], in_=ident[:].rearrange("p (n g u) -> p u n g", n=SAMPLES, u=2)
        )
        perm_halves = perm[:].rearrange("p u n g -> p u (n g)")

        ones = const.tile([P, 1], F32)
        nc.vector.memset(ones[:], 1.0)
        table_warmer = const.tile([P, 1], F32)
        nc.scalar.sqrt(out=table_warmer[:], in_=ones[:])

        vectors = (
            (img_b, img_gamma, img_beta, img_mean, img_var),
            (pts_b, pts_gamma, pts_beta, pts_mean, pts_var),
        )
        vec_rows = const.tile([P, P], BF16)
        nc.gpsimd.memset(vec_rows[:], 0.0)
        for b in range(2):
            for v in range(5):
                row = (b * 5 + v) * O_HALVES
                nc.gpsimd.dma_start(
                    out=vec_rows[row : row + O_HALVES, :],
                    in_=vectors[b][v].rearrange("(h o) -> h o", h=O_HALVES),
                )

        l3_rows = img.tile([P, RUN], BF16)
        nc.sync.dma_start(
            out=l3_rows[:], in_=img_feat3.rearrange("n (m q) h w -> (n m) (q h w)", q=RUN)
        )
        l4_rows = img.tile([P, RUN], BF16)
        nc.sync.dma_start(
            out=l4_rows[:], in_=img_feat4.rearrange("n (m q) h w -> (n m) (q h w)", q=RUN)
        )
        l2_rows = img.tile([P, RUN, L2_W], BF16)
        nc.sync.dma_start(
            out=l2_rows[:], in_=img_feat2.rearrange("n (m q) h w -> (n m) q (h w)", q=RUN)
        )
        l1_rows = img.tile([P, RUN, L1_H * L1_W], BF16)
        nc.sync.dma_start(
            out=l1_rows[:], in_=img_feat1.rearrange("n (m q) h w -> (n m) q (h w)", q=RUN)
        )
        l0_rows = img.tile([P, RUN, GRID], BF16)

        lower = img.tile([P, RUN, L1_H, L1_W], F32)
        lower_t = img.tile([P, L1_H, L1_W, SAMPLES, PASSES, PACK], F32)
        img_cols = SAMPLES * GRID
        img_grouped = img.tile([P, PASSES, img_cols, PACK], BF16, align_bytes=64)
        img_codes = img.tile([P, PASSES * img_cols + MIN_MOVING - img_cols], U32, align_bytes=64)
        img_scales = img.tile([P, PASSES * img_cols + MIN_MOVING - img_cols], U8, align_bytes=64)
        nc.gpsimd.memset(img_codes[:, PASSES * img_cols :].bitcast(I32), 0)
        nc.gpsimd.memset(img_scales[:, PASSES * img_cols :].bitcast(I32), 0)
        img_w_codes = img.tile([P, PASSES, OUT_CH], U32, align_bytes=64)
        img_w_scales = img.tile([P, PASSES, OUT_CH], U8, align_bytes=64)

        def add_lower_levels():
            sum34 = img.tile([P, RUN], F32)
            nc.vector.tensor_tensor(out=sum34[:], in0=l3_rows[:], in1=l4_rows[:], op=ADD)
            sum234 = img.tile([P, RUN, L2_W], F32)
            nc.vector.tensor_tensor(
                out=sum234[:],
                in0=l2_rows[:],
                in1=sum34[:].unsqueeze(2).to_broadcast([P, RUN, L2_W]),
                op=ADD,
            )
            l1_view = l1_rows[:].rearrange("p q (r d k) -> p q r d k", r=L1_H, d=L2_W)
            for r in range(L1_H):
                nc.vector.tensor_tensor(
                    out=lower[:, :, r].rearrange("p q (d k) -> p q d k", d=L2_W),
                    in0=l1_view[:, :, r],
                    in1=sum234[:].unsqueeze(3).to_broadcast([P, RUN, L2_W, L1_W // L2_W]),
                    op=ADD,
                )

        def transpose_lower_levels():
            lower_words = lower[:].rearrange("p (x e) r c -> p r c e x", e=2)
            for r in range(L1_H):
                for d in range(L2_W):
                    lower_bank = banks.tile([P, 2, 2, P], F32, tag="bank")
                    for k in range(2):
                        for e in range(2):
                            nc.tensor.transpose(
                                lower_bank[:, k, e, :], lower_words[:, r, 2 * d + k, e, :], ident[:]
                            )
                    nc.scalar.copy(
                        out=lower_t[:, r, 2 * d : 2 * d + 2].rearrange(
                            "p k n g (u e) -> p k (n g u) e", e=2
                        ),
                        in_=lower_bank[:].rearrange("p k e q -> p k q e"),
                    )

        l0_banks = {}

        def transpose_level0_row(i):
            l0_words = l0_rows[:].bitcast(F32).rearrange("p (x e) (i k) -> p e i k x", e=2, i=GRID_H)
            for quad in range(2):
                bank = grids.tile([P, 2, 2, 2, SAMPLES * PASSES], F32, tag="img_sum%d" % quad, name="l0_bank%d" % quad)
                for k in range(2):
                    for e in range(2):
                        nc.tensor.transpose(
                            bank[:, :, e, k, :], l0_words[:, e, i, 2 * quad + k, :], perm_halves
                        )
                l0_banks[i, quad] = bank

        def add_grid_row(i):
            for k in range(GRID_W // 2):
                values = l0_banks[i, k // 2][:].bitcast(BF16)
                for n in range(SAMPLES):
                    r = padded_source(GRID_TOP + i, TH, L1_H, n + 1)
                    c0 = padded_source(GRID_LEFT + 2 * k, TW, L1_W, n + 1)
                    c1 = padded_source(GRID_LEFT + 2 * k + 1, TW, L1_W, n + 1)
                    if c0 == c1:
                        lower_pair = (
                            lower_t[:, r, c0, n].unsqueeze(3).to_broadcast([P, PASSES, PACK, 2])
                        )
                    else:
                        assert c1 == c0 + 1
                        lower_pair = lower_t[:, r, c0 : c1 + 1, n].rearrange("p c g t -> p g t c")
                    first = n * GRID + i * GRID_W + 2 * k
                    nc.vector.tensor_tensor(
                        out=img_grouped[:, :, first : first + 2, :].rearrange("p g s t -> p g t s"),
                        in0=values[:, :, :, k % 2, n * 2 * PASSES : (n + 1) * 2 * PASSES].rearrange(
                            "p u e (g s) -> p g (u e) s", s=2
                        ),
                        in1=lower_pair,
                        op=ADD,
                    )

        def quantise_img_m():
            half = PASSES // 2
            for part in range(2):
                cols = slice(part * half * img_cols, (part + 1) * half * img_cols)
                nc.vector.quantize_mx(
                    out=img_codes[:, cols].bitcast(FP8X4),
                    scales=img_scales[:, cols],
                    in_=img_grouped[:, part * half : (part + 1) * half].rearrange(
                        "p g c t -> p (g c t)"
                    ),
                )

        def prepare_img(chunk):
            w_raw = load_weight_chunk(nc, w_in, img_w, chunk)
            if chunk == CHUNKS - 1:
                raw[7] = load_weight_chunk(nc, w_in, pts_w, 7)
            w_grouped = transpose_weight_chunk(nc, banks, work, ident, w_raw, WORDS_IN_HALVES)
            passes = slice(chunk * CHUNK_PASSES, (chunk + 1) * CHUNK_PASSES)
            quantise_chunk(nc, w_grouped[:], img_w_codes[:, passes], img_w_scales[:, passes])

        bn = {}

        def widen_vectors():
            vec_rows_f32 = const.tile([P, P], F32)
            nc.gpsimd.tensor_copy(out=vec_rows_f32[:], in_=vec_rows[:])
            bn["rows"] = vec_rows_f32

        def transpose_vectors():
            vec_bank = banks.tile([P, O_HALVES, 2, P], F32, tag="bank")
            nc.tensor.transpose(vec_bank[:, 0, 0, :], bn["rows"][:], ident[:])
            vec = const.tile([P, 2, 5, O_HALVES], F32)
            nc.scalar.copy(
                out=vec[:].rearrange("p b v h -> p (b v h)"),
                in_=vec_bank[:, 0, 0, 0 : 2 * 5 * O_HALVES],
            )
            bn["vec"] = vec

        def raise_variance():
            var_eps = const.tile([P, 2, O_HALVES], F32)
            nc.gpsimd.tensor_scalar_add(out=var_eps[:], in0=bn["vec"][:, :, 4, :], scalar1=BN_EPS)
            bn["var_eps"] = var_eps

        def take_root():
            std = const.tile([P, 2, O_HALVES], F32)
            nc.scalar.sqrt(out=std[:], in_=bn["var_eps"][:])
            bn["std"] = std

        def fold_batch_norm():
            bias, gamma, beta, mean = (bn["vec"][:, :, v, :] for v in range(4))
            inv_std = const.tile([P, 2, O_HALVES], F32)
            nc.vector.reciprocal(out=inv_std[:], in_=bn["std"][:])
            bn_scale = const.tile([P, 2, O_HALVES], F32)
            nc.gpsimd.tensor_mul(out=bn_scale[:], in0=gamma, in1=inv_std[:])
            centred = const.tile([P, 2, O_HALVES], F32)
            nc.gpsimd.tensor_sub(out=centred[:], in0=bias, in1=mean)
            scaled = const.tile([P, 2, O_HALVES], F32)
            nc.gpsimd.tensor_mul(out=scaled[:], in0=centred[:], in1=bn_scale[:])
            bn_shift = const.tile([P, 2, O_HALVES], F32)
            nc.gpsimd.tensor_add(out=bn_shift[:], in0=scaled[:], in1=beta)
            bn["scale"], bn["shift"] = bn_scale, bn_shift

        img_sums = []

        def multiply_img(chunk):
            for h in range(O_HALVES):
                o_cols = slice(h * P, (h + 1) * P)
                for g in range(chunk * CHUNK_PASSES, (chunk + 1) * CHUNK_PASSES):
                    moving = slice(g * img_cols, g * img_cols + MIN_MOVING)
                    nc.tensor.matmul_mx(
                        out=img_sums[h][:],
                        lhsT=img_w_codes[:, g, o_cols].bitcast(FP8X4),
                        lhsT_scale=img_w_scales[:, g, o_cols],
                        rhs=img_codes[:, moving].bitcast(FP8X4),
                        rhs_scale=img_scales[:, moving],
                        start=(g == 0),
                        stop=(g == PASSES - 1),
                    )

        img_results = []

        def finish_img():
            for h in range(O_HALVES):
                grid = img_sums[h][:, 0:img_cols].rearrange(
                    "p (n i j) -> p n i j", n=SAMPLES, i=GRID_H
                )
                img_res = results.tile([P, SAMPLES, TH, TW], F32)
                rows = slice(GRID_TOP, GRID_TOP + GRID_H)
                right = GRID_LEFT + GRID_W
                for dst_cols, src in (
                    (slice(GRID_LEFT, right), grid),
                    (slice(0, GRID_LEFT), grid[:, :, :, 0:1]),
                    (slice(right, TW), grid[:, :, :, GRID_W - 1 : GRID_W]),
                ):
                    dst = img_res[:, :, rows, dst_cols]
                    nc.scalar.activation(
                        out=dst,
                        in_=src.to_broadcast(dst.shape),
                        func=RELU,
                        bias=bn["shift"][:, 0, h : h + 1],
                        scale=bn["scale"][:, 0, h : h + 1],
                    )
                nc.scalar.copy(
                    out=img_res[:, :, 0:GRID_TOP, :],
                    in_=img_res[:, :, GRID_TOP : GRID_TOP + 1, :].to_broadcast(
                        [P, SAMPLES, GRID_TOP, TW]
                    ),
                )
                bottom = GRID_TOP + GRID_H
                nc.scalar.copy(
                    out=img_res[:, :, bottom:TH, :],
                    in_=img_res[:, :, bottom - 1 : bottom, :].to_broadcast(
                        [P, SAMPLES, TH - bottom, TW]
                    ),
                )
                img_results.append(img_res)

        def store_img():
            for h in range(O_HALVES):
                nc.sync.dma_start(
                    out=out[:, h * P : (h + 1) * P].rearrange("n o h w -> o n (h w)"),
                    in_=img_results[h][:].rearrange("p n h w -> p n (h w)"),
                )

        pts_sums = [
            sums.tile([P, SAMPLES * POSITIONS], F32, name="pts_sum%d" % h) for h in range(O_HALVES)
        ]
        operands = {}

        raw = {}

        def prepare_pts(chunk, parts):
            w_raw = raw[chunk] if chunk in raw else load_weight_chunk(nc, w_in, pts_w, chunk)
            pts_raw = pts_in.tile([P, SAMPLES, CHUNK_PASSES * PACK, POSITIONS], BF16)
            for passes in parts:
                load_pts_passes(nc, pts_raw, pts_feat0, chunk, passes)
            w_grouped = transpose_weight_chunk(nc, banks, work, ident, w_raw, WORDS_ALTERNATING)
            w_codes = coded.tile([P, CHUNK_PASSES, OUT_CH], U32, align_bytes=64)
            w_scales = coded.tile([P, CHUNK_PASSES, OUT_CH], U8, align_bytes=64)
            pts_grouped = single.tile(
                [P, CHUNK_PASSES, SAMPLES * POSITIONS, PACK], BF16, align_bytes=64
            )
            pts_codes = coded.tile([P, CHUNK_PASSES, SAMPLES * POSITIONS], U32, align_bytes=64)
            pts_scales = coded.tile([P, CHUNK_PASSES, SAMPLES * POSITIONS], U8, align_bytes=64)
            for number, passes in enumerate(parts):
                regroup_pts_passes(nc, pts_grouped, pts_raw, passes, VSHARE[chunk])
                if number == 0:
                    quantise_chunk(nc, w_grouped[:], w_codes[:], w_scales[:])
                quantise_chunk(
                    nc, pts_grouped[:, passes], pts_codes[:, passes], pts_scales[:, passes]
                )
            operands[chunk] = (w_codes, w_scales, pts_codes, pts_scales)

        def multiply_pts(chunk, passes=slice(0, CHUNK_PASSES)):
            w_codes, w_scales, pts_codes, pts_scales = operands[chunk]
            for g in range(passes.start, passes.stop):
                done = chunk * CHUNK_PASSES + g
                for h in range(O_HALVES):
                    o_cols = slice(h * P, (h + 1) * P)
                    nc.tensor.matmul_mx(
                        out=pts_sums[h][:],
                        lhsT=w_codes[:, g, o_cols].bitcast(FP8X4),
                        lhsT_scale=w_scales[:, g, o_cols],
                        rhs=pts_codes[:, g, :].bitcast(FP8X4),
                        rhs_scale=pts_scales[:, g, :],
                        start=(done == 0),
                        stop=(done == PASSES - 1),
                    )

        whole = [slice(0, CHUNK_PASSES)]
        last = [slice(0, 2), slice(2, 3), slice(3, 4)]
        raw[0] = load_weight_chunk(nc, w_in, pts_w, 0)
        add_lower_levels()
        prepare_pts(0, whole)
        transpose_lower_levels()
        nc.sync.dma_start(
            out=l0_rows[:], in_=img_feat0.rearrange("n (m q) h w -> (n m) q (h w)", q=RUN)
        )
        done_img = 0
        for number, (branch, chunk) in enumerate(ITEMS):
            if number in ROW_T:
                transpose_level0_row(ROW_T[number])
            if number in ROW_A:
                add_grid_row(ROW_A[number])
            if branch == "img":
                prepare_img(chunk)
            else:
                prepare_pts(chunk, whole if chunk < CHUNKS - 1 else last)
            if number == QIMG:
                quantise_img_m()
                img_sums += [
                    grids.tile([P, MIN_MOVING], F32, tag="img_sum%d" % h, name="img_sum%d" % h)
                    for h in range(O_HALVES)
                ]
            if number == 7:
                widen_vectors()
            if number == 9:
                transpose_vectors()
            if number == 10:
                raise_variance()
            if number == 11:
                take_root()
            if number == 12:
                fold_batch_norm()
            if number in (1, 2):
                multiply_pts(0, slice(2 * number - 2, 2 * number))
            if number >= 4:
                back = 2 if ITEMS[number - 2][0] == "pts" else 3
                multiply_pts(ITEMS[number - back][1], slice(2 * back - 4, 2 * back - 2))
            for c in MIMG.get(number, ()):
                multiply_img(c)
        multiply_pts(CHUNKS - 2, slice(2, 4))
        multiply_img(7)
        finish_img()
        store_img()
        multiply_pts(CHUNKS - 1)

        for h in range(O_HALVES):
            pts_res = results.tile([P, SAMPLES, POSITIONS], F32)
            nc.scalar.activation(
                out=pts_res[:].rearrange("p n s -> p (n s)"),
                in_=pts_sums[h][:],
                func=RELU,
                bias=bn["shift"][:, 1, h : h + 1],
                scale=bn["scale"][:, 1, h : h + 1],
            )
            store_queue = nc.sync if h == 0 else nc.scalar
            store_queue.dma_start(
                out=out[:, OUT_CH + h * P : OUT_CH + (h + 1) * P].rearrange("n o h w -> o n (h w)"),
                in_=pts_res[:],
            )
